import numpy as np
import ml_dtypes


def mxq(x, axis, fmt="e4m3"):
    dtype, down = {"e4m3": (ml_dtypes.float8_e4m3fn, 7), "e5m2": (ml_dtypes.float8_e5m2, 14)}[fmt]
    v = np.moveaxis(np.asarray(x, np.float32).astype(ml_dtypes.bfloat16).astype(np.float64), axis, -1)
    blocks = v.reshape(v.shape[:-1] + (-1, 32))
    amax = np.abs(blocks).max(-1, keepdims=True)
    byte = np.maximum(np.where(amax > 0, np.frexp(amax)[1] - 1 + 127, 0) - down, 1)
    scale = np.exp2(byte - 127.0)
    codes = (blocks / scale).astype(np.float32).astype(dtype).astype(np.float64)
    return np.moveaxis((codes * scale).reshape(v.shape), -1, axis)


WIDE = False


def mx_kscale(k):
    if not WIDE:
        return np.ones(k)
    levels = np.array([10, -10, 5, -5, 0])
    if k % 512:
        return np.exp2(np.random.permutation(np.resize(levels, k // 32))).repeat(32)
    a = np.empty((k // 512, 16))
    for p in range(k // 512):
        a[p, :8] = np.random.permutation(np.resize(levels, 8))
        for g in range(8):
            far = levels[np.abs(levels - a[p, g]) >= 10]
            a[p, g + 8] = far[np.random.randint(len(far))]
    return np.exp2(a.ravel()).repeat(32)


BF16 = ml_dtypes.bfloat16


def bf(x):
    return np.asarray(x, np.float32).astype(BF16)


def f64(x):
    return np.asarray(x).astype(np.float64)


N, E, C, D1, D2 = 512, 2048, 512, 2, 2
T1 = D1 + 1


def shift_down(y, k):
    return np.pad(y, ((k, 0), (0, 0)))[:y.shape[0]] if k > 0 else y


def shift_up(y, k):
    return np.pad(y, ((0, k), (0, 0)))[k:] if k > 0 else y


def setup_inputs():
    s = np.asarray(mx_kscale(N))
    u = np.asarray(mx_kscale(C))
    t = np.maximum.reduce([s[np.maximum(np.arange(N) - k, 0)] for k in range(T1)])
    x0 = bf(np.random.standard_normal((N, E)))
    W0 = bf(np.random.standard_normal((T1, E, C)) * 0.4 / np.sqrt(E))
    b1 = bf(np.random.standard_normal((1, C)) * 0.25)
    g = bf(np.random.standard_normal((N, C)) * np.exp2(np.random.randint(-6, 1, (N, 1))) * 4.0 / t[:, None] * u)
    Y = f64(x0) @ f64(W0)
    cnt1 = np.minimum(np.arange(N), D1) + 1.0
    z = sum(shift_down(Y[k], k) for k in range(T1)) + cnt1[:, None] * f64(b1)[0]
    return {"x": bf(f64(x0) * s[:, None]), "W1": bf(f64(W0) / u), "b1": b1,
            "z": np.asarray(z, np.float32), "grad_out": g}


def reference(x, W1, b1, z, grad_out):
    th = np.tanh(f64(z))
    dz = f64(grad_out) * (1.0 - th * th)
    P = mxq(dz, 1, "e5m2") @ mxq(f64(W1), 2, "e4m3").transpose(0, 2, 1)
    dx = sum(shift_up(P[k], k) for k in range(T1))
    D = np.stack([shift_up(dz, k) for k in range(T1)])
    dW = mxq(f64(x), 0, "e4m3").T @ mxq(D, 1, "e5m2")
    return dx, dW

@@ -1,0 +1,314 @@
+from contextlib import ExitStack
+
+import concourse.mybir as mybir
+from concourse.masks import make_identity
+
+N_TOK, E, C, TAPS = 512, 2048, 512, 3
+FLOPS = 2 * 2 * TAPS * N_TOK * E * C
+
+F32 = mybir.dt.float32
+BF16 = mybir.dt.bfloat16
+U32 = mybir.dt.uint32
+U8 = mybir.dt.uint8
+E4M3 = mybir.dt.float8_e4m3fn_x4
+E5M2 = mybir.dt.float8_e5m2_x4
+ACT = mybir.ActivationFunctionType
+ALU = mybir.AluOpType
+
+P = 128
+
+LOADS = (
+    ("g",), ("z", 0), ("z", 1), ("w", 0, 0), ("w", 1, 0),
+    ("w", 2, 0), ("x", 0), ("x", 1), ("w", 0, 1), ("w", 1, 1),
+    ("w", 2, 1),
+)
+PLAN = (
+    ("Wt", 0, 0), ("Wc", 0, 0, "S"), ("Wt", 0, 1), ("Wc", 0, 1, "S"), ("SH",),
+    ("Ft", 0), ("Ft", 2), ("D", 0, "V"), ("Fc", 0), ("Fc", 4),
+    ("Fc", 2), ("Wt", 1, 0), ("Wc", 1, 0, "S"), ("Wt", 1, 1), ("Wc", 1, 1, "S"),
+    ("Wq", 0, 0), ("Wq", 0, 1), ("qF",), ("Wt", 2, 0), ("Wc", 2, 0, "S"),
+    ("Wt", 2, 1), ("Wc", 2, 1, "S"), ("Wq", 1, 0), ("Wq", 1, 1), ("Wq", 2, 0),
+    ("Wq", 2, 1), ("M0", 0, 0), ("qD", 0), ("E0", 0, 0, "SSSS"), ("X", 0, "V"),
+    ("D", 1, "V"), ("qX", 0), ("M0", 0, 1), ("D", 2, "V"), ("E0", 0, 1, "SSSS"),
+    ("qD", 1), ("qD", 2), ("M1", 0, 0), ("E1", 0, 0, "SSVS"), ("X", 1, "V"),
+    ("M1", 1, 0), ("E1", 1, 0, "SVSS"), ("qX", 1), ("M1", 2, 0), ("E1", 2, 0, "SVSV"),
+    ("Wt", 0, 2), ("Wc", 0, 2, "S"), ("Wt", 0, 3), ("Wc", 0, 3, "S"), ("M1", 0, 1),
+    ("E1", 0, 1, "SVSV"), ("Wq", 0, 2), ("Wq", 0, 3), ("M1", 1, 1), ("E1", 1, 1, "SVSV"),
+    ("X", 2, "V"), ("Wt", 1, 2), ("Wc", 1, 2, "S"), ("Wt", 1, 3), ("Wc", 1, 3, "S"),
+    ("M1", 2, 1), ("E1", 2, 1, "SVSV"), ("qX", 2), ("Wq", 1, 2), ("Wq", 1, 3),
+    ("M1", 0, 2), ("E1", 0, 2, "SVSV"), ("X", 3, "V"), ("Wt", 2, 2), ("Wc", 2, 2, "S"),
+    ("Wt", 2, 3), ("Wc", 2, 3, "S"), ("M1", 1, 2), ("E1", 1, 2, "SVSV"), ("qX", 3),
+    ("Wq", 2, 2), ("Wq", 2, 3), ("M1", 2, 2), ("E1", 2, 2, "SVSV"), ("M1", 0, 3),
+    ("E1", 0, 3, "SVSV"), ("M0", 1, 0), ("E0", 1, 0, "SVSV"), ("M1", 1, 3), ("E1", 1, 3, "SVSV"),
+    ("M0", 1, 1), ("E0", 1, 1, "SVSV"), ("M1", 2, 3), ("E1", 2, 3, "SVSV"),
+)
+
+
+def tile_predictor_pa_v_kernel(tc, x, W1, b1, z, grad_out, out_0, out_1):
+    nc = tc.nc
+    with ExitStack() as ctx:
+        ctx.enter_context(tc.manual_schedule())
+        const = ctx.enter_context(tc.tile_pool(name="const", bufs=1))
+        head = ctx.enter_context(tc.tile_pool(name="head", bufs=1))
+        keep = ctx.enter_context(tc.tile_pool(name="keep", bufs=1))
+        grp = ctx.enter_context(tc.tile_pool(name="grp", bufs=5))
+        stage = ctx.enter_context(tc.tile_pool(name="stage", bufs=6))
+        tp = ctx.enter_context(tc.psum_pool(name="tp", bufs=4))
+        acc = ctx.enter_context(tc.psum_pool(name="acc", bufs=4))
+
+        engines = {"S": nc.scalar.copy, "V": nc.vector.tensor_copy}
+
+        g_sb = head.tile([P, 4, C], BF16, name="g_sb")
+        z_view = z.rearrange("(p j) c -> p j c", j=4)
+        x_view = x.rearrange("(p j) e -> p j e", j=4)
+        z_sb = {}
+        x_sb = {}
+        w_sb = {}
+
+        def load_g():
+            nc.sync.dma_start(out=g_sb[:], in_=grad_out.rearrange("(p j) c -> p j c", j=4))
+
+        def load_z(i):
+            zt = head.tile([P, 2, C], F32, name="z%d" % i)
+            nc.sync.dma_start(out=zt[:], in_=z_view[:, 2 * i : 2 * i + 2, :])
+            z_sb[i] = zt
+
+        def load_x(h):
+            xt = keep.tile([P, 4, 1024], BF16, name="x%d" % h)
+            nc.sync.dma_start(out=xt[:], in_=x_view[:, :, 1024 * h : 1024 * (h + 1)])
+            x_sb[h] = xt
+
+        def load_w(k, h):
+            wt = keep.tile([P, 2, 4, C], BF16, name="w%d%d" % (k, h))
+            nc.sync.dma_start(
+                out=wt[:],
+                in_=W1[k, 1024 * h : 1024 * (h + 1), :].rearrange("(b m t) c -> m b t c", b=2, t=4),
+            )
+            w_sb[(k, h)] = wt
+
+        for step in LOADS:
+            if step[0] == "g":
+                load_g()
+            elif step[0] == "z":
+                load_z(step[1])
+            elif step[0] == "x":
+                load_x(step[1])
+            else:
+                load_w(step[1], step[2])
+
+        warm = const.tile([P, 8], F32, name="warm")
+        nc.vector.memset(warm[:], 0.0)
+        nc.scalar.activation(out=warm[:], in_=warm[:], func=ACT.Tanh)
+        ident = const.tile([P, P], F32, name="ident")
+        make_identity(nc, ident[:])
+        shift_b = const.tile([P, P], BF16, name="shift_b")
+        nc.vector.memset(shift_b[:], 0.0)
+        nc.vector.tensor_copy(out=shift_b[:, 0 : P - 1], in_=ident[:, 1:P])
+
+        dzb = keep.tile([P, 6, C], BF16, name="dzb")
+        ng = head.tile([P, 4, C], BF16, name="ng")
+        nc.gpsimd.tensor_scalar(out=ng[:], in0=g_sb[:], scalar1=-1.0, scalar2=0.0, op0=ALU.mult, op1=ALU.add)
+        th = []
+        for i in range(2):
+            tt = head.tile([P, 2, C], F32, name="th%d" % i)
+            nc.scalar.activation(out=tt[:], in_=z_sb[i][:], func=ACT.Tanh)
+            th.append(tt)
+        nc.vector.tensor_tensor(out=th[0][:], in0=th[0][:], in1=th[0][:], op=ALU.mult)
+        nc.scalar.activation(out=th[1][:], in_=th[1][:], func=ACT.Square)
+        for i in range(2):
+            nc.vector.scalar_tensor_tensor(
+                out=dzb[:, 2 * i : 2 * i + 2, :],
+                in0=th[i][:],
+                scalar=1.0,
+                in1=ng[:, 2 * i : 2 * i + 2, :],
+                op0=ALU.subtract,
+                op1=ALU.mult,
+            )
+
+        xq = keep.tile([P, E], U32, name="xq", align_bytes=64)
+        xs = keep.tile([P, E], U8, name="xs", align_bytes=64)
+        wq = []
+        ws = []
+        dq = []
+        ds = []
+        for k in range(TAPS):
+            wqk = keep.tile([P, E], U32, name="wq%d" % k, align_bytes=64)
+            wsk = keep.tile([P, E], U8, name="ws%d" % k, align_bytes=64)
+            dqk = keep.tile([P, C], U32, name="dq%d" % k, align_bytes=64)
+            dsk = keep.tile([P, C], U8, name="ds%d" % k, align_bytes=64)
+            wq.append(wqk)
+            ws.append(wsk)
+            dq.append(dqk)
+            ds.append(dsk)
+        fq = keep.tile([P, 6 * P], U32, name="fq", align_bytes=64)
+        fs = keep.tile([P, 6 * P], U8, name="fs", align_bytes=64)
+        gf = keep.tile([P, 6 * P * 4], BF16, name="gf", align_bytes=64)
+        gf_words = gf[:].bitcast(F32).rearrange("p (s n u) -> p s n u", s=6, u=2)
+
+        banks = {}
+        groups = {}
+
+        def shift_rows():
+            sh = tp.tile([P, 2 * C], BF16, name="sh", tag="tp")
+            for j in range(2):
+                nc.tensor.matmul(out=sh[:, C * j : C * (j + 1)], lhsT=shift_b[:], rhs=dzb[:, j, :], start=True, stop=True)
+            nc.scalar.copy(out=dzb[:, 4:6, :], in_=sh[:].rearrange("p (j c) -> p j c", j=2))
+
+        nc.vector.memset(gf[:].rearrange("p (s n t) -> p s n t", s=6, t=4)[:, 4:6, P - 1, :], 0.0)
+
+        def f_transpose(s0):
+            bank = tp.tile([P, 4 * P], F32, name="ft", tag="tp")
+            for sl in range(2):
+                words = dzb[:, s0 + sl, :].bitcast(F32)
+                for u in range(2):
+                    q = 2 * sl + u
+                    nc.tensor.transpose(bank[:, P * q : P * (q + 1)], words[:, u : C // 2 : 2], ident[:])
+            banks[("F", s0)] = bank
+
+        def f_copy(s0):
+            src = banks[("F", s0 % 4)][:].rearrange("p (s u n) -> p s n u", s=2, u=2)
+            if s0 < 4:
+                nc.vector.tensor_copy(out=gf_words[:, s0 : s0 + 2, :, :], in_=src)
+            else:
+                nc.vector.tensor_copy(out=gf_words[:, s0 : s0 + 2, 0 : P - 1, :], in_=src[:, :, 1:P, :])
+
+        def f_quant():
+            nc.vector.quantize_mx(out=fq[:, 0:512].bitcast(E5M2), scales=fs[:, 0:512], in_=gf[:, 0:2048])
+            nc.vector.quantize_mx(out=fq[:, 512:768].bitcast(E5M2), scales=fs[:, 512:768], in_=gf[:, 2048:3072])
+
+        def d_group(k, eng):
+            g = grp.tile([P, 4 * C], BF16, name="gd", tag="grp", align_bytes=64)
+            engines[eng](out=g[:].rearrange("p (c t) -> p c t", t=4), in_=dzb[:, k : k + 4, :].rearrange("p t c -> p c t"))
+            groups[("D", k)] = g
+
+        def d_quant(k):
+            nc.vector.quantize_mx(out=dq[k][:].bitcast(E5M2), scales=ds[k][:], in_=groups[("D", k)][:])
+
+        def x_group(b, eng):
+            g = grp.tile([P, 4 * 512], BF16, name="gx", tag="grp", align_bytes=64)
+            src = x_sb[b // 2][:, :, 512 * (b % 2) : 512 * (b % 2 + 1)]
+            engines[eng](
+                out=g[:].rearrange("p (t m j) -> p t m j", t=4, j=4),
+                in_=src.rearrange("p j (m t) -> p t m j", t=4),
+            )
+            groups[("X", b)] = g
+
+        def x_quant(b):
+            cols = slice(512 * b, 512 * (b + 1))
+            nc.vector.quantize_mx(out=xq[:, cols].bitcast(E4M3), scales=xs[:, cols], in_=groups[("X", b)][:])
+
+        def w_transpose(k, bb):
+            pair = []
+            for half in range(2):
+                bank = tp.tile([P, 4 * P], F32, name="wt", tag="tp")
+                for tl in range(2):
+                    words = w_sb[(k, bb // 2)][:, bb % 2, 2 * half + tl, :].bitcast(F32)
+                    for u in range(2):
+                        q = 2 * tl + u
+                        nc.tensor.transpose(bank[:, P * q : P * (q + 1)], words[:, u : C // 2 : 2], ident[:])
+                pair.append(bank)
+            banks[(k, bb)] = pair
+
+        def w_copy(k, bb, eng):
+            g = grp.tile([P, 4 * 512], BF16, name="gw", tag="grp", align_bytes=64)
+            words = g[:].bitcast(F32).rearrange("p (m t u) -> p m t u", t=4, u=2)
+            for half in range(2):
+                engines[eng](
+                    out=words[:, :, 2 * half : 2 * half + 2, :],
+                    in_=banks[(k, bb)][half][:].rearrange("p (t u m) -> p m t u", t=2, u=2),
+                )
+            groups[("W", k, bb)] = g
+
+        def w_quant(k, bb):
+            cols = slice(512 * bb, 512 * (bb + 1))
+            nc.vector.quantize_mx(out=wq[k][:, cols].bitcast(E4M3), scales=ws[k][:, cols], in_=groups[("W", k, bb)][:])
+
+        def out1_mm(k, b):
+            accs = []
+            for t in range(4):
+                a = acc.tile([P, C], F32, name="acc", tag="acc")
+                cols = slice(512 * b + P * t, 512 * b + P * (t + 1))
+                nc.tensor.matmul_mx(
+                    out=a[:],
+                    lhsT=xq[:, cols].bitcast(E4M3),
+                    lhsT_scale=xs[:, cols],
+                    rhs=dq[k][:].bitcast(E5M2),
+                    rhs_scale=ds[k][:],
+                    start=True,
+                    stop=True,
+                )
+                accs.append(a)
+            banks[("O1", k, b)] = accs
+
+        def out1_store(k, b, pattern):
+            st = stage.tile([P, 4, C], F32, name="st", tag="st")
+            accs = banks[("O1", k, b)]
+            dst = out_1[k, 512 * b : 512 * (b + 1), :].rearrange("(m t) c -> m t c", t=4)
+            for t in range(4):
+                engines[pattern[t]](out=st[:, t, :], in_=accs[t][:])
+            nc.sync.dma_start(out=dst, in_=st[:])
+
+        out_0_view = out_0.rearrange("(n j) e -> n j e", j=4)
+
+        def out0_mm(h, jp):
+            accs = []
+            for q in range(4):
+                j = 2 * jp + q // 2
+                bb = 2 * h + q % 2
+                a = acc.tile([P, 512], F32, name="acc", tag="acc")
+                ecols = slice(512 * bb, 512 * (bb + 1))
+                for k in range(TAPS):
+                    tcols = slice(P * (j + k), P * (j + k + 1))
+                    nc.tensor.matmul_mx(
+                        out=a[:],
+                        lhsT=fq[:, tcols].bitcast(E5M2),
+                        lhsT_scale=fs[:, tcols],
+                        rhs=wq[k][:, ecols].bitcast(E4M3),
+                        rhs_scale=ws[k][:, ecols],
+                        start=(k == 0),
+                        stop=(k == TAPS - 1),
+                    )
+                accs.append(a)
+            banks[("O0", h, jp)] = accs
+
+        def out0_store(h, jp, pattern):
+            st = stage.tile([P, 2, 1024], F32, name="st", tag="st")
+            accs = banks[("O0", h, jp)]
+            for q in range(4):
+                engines[pattern[q]](out=st[:, q // 2, 512 * (q % 2) : 512 * (q % 2 + 1)], in_=accs[q][:])
+            nc.sync.dma_start(out=out_0_view[:, 2 * jp : 2 * jp + 2, 1024 * h : 1024 * (h + 1)], in_=st[:])
+
+        for step in PLAN:
+            kind = step[0]
+            if kind == "SH":
+                shift_rows()
+            elif kind == "Ft":
+                f_transpose(step[1])
+            elif kind == "Fc":
+                f_copy(step[1])
+            elif kind == "qF":
+                f_quant()
+            elif kind == "D":
+                d_group(step[1], step[2])
+            elif kind == "qD":
+                d_quant(step[1])
+            elif kind == "X":
+                x_group(step[1], step[2])
+            elif kind == "qX":
+                x_quant(step[1])
+            elif kind == "Wt":
+                w_transpose(step[1], step[2])
+            elif kind == "Wc":
+                w_copy(step[1], step[2], step[3])
+            elif kind == "Wq":
+                w_quant(step[1], step[2])
+            elif kind == "M1":
+                out1_mm(step[1], step[2])
+            elif kind == "E1":
+                out1_store(step[1], step[2], step[3])
+            elif kind == "M0":
+                out0_mm(step[1], step[2])
+            elif kind == "E0":
+                out0_store(step[1], step[2], step[3])
+            else:
+                raise ValueError(kind)

@@ -23,24 +23,25 @@ LOADS = (
     ("w", 2, 1),
 )
 PLAN = (
-    ("Wt", 0, 0), ("Wc", 0, 0, "S"), ("Wt", 0, 1), ("Wc", 0, 1, "S"), ("SH",),
-    ("Ft", 0), ("Ft", 2), ("D", 0, "V"), ("Fc", 0), ("Fc", 4),
-    ("Fc", 2), ("Wt", 1, 0), ("Wc", 1, 0, "S"), ("Wt", 1, 1), ("Wc", 1, 1, "S"),
-    ("Wq", 0, 0), ("Wq", 0, 1), ("qF",), ("Wt", 2, 0), ("Wc", 2, 0, "S"),
-    ("Wt", 2, 1), ("Wc", 2, 1, "S"), ("Wq", 1, 0), ("Wq", 1, 1), ("Wq", 2, 0),
-    ("Wq", 2, 1), ("M0", 0, 0), ("qD", 0), ("E0", 0, 0, "SSSS"), ("X", 0, "V"),
-    ("D", 1, "V"), ("qX", 0), ("M0", 0, 1), ("D", 2, "V"), ("E0", 0, 1, "SSSS"),
-    ("qD", 1), ("qD", 2), ("M1", 0, 0), ("E1", 0, 0, "SSVS"), ("X", 1, "V"),
-    ("M1", 1, 0), ("E1", 1, 0, "SVSS"), ("qX", 1), ("M1", 2, 0), ("E1", 2, 0, "SVSV"),
-    ("Wt", 0, 2), ("Wc", 0, 2, "S"), ("Wt", 0, 3), ("Wc", 0, 3, "S"), ("M1", 0, 1),
-    ("E1", 0, 1, "SVSV"), ("Wq", 0, 2), ("Wq", 0, 3), ("M1", 1, 1), ("E1", 1, 1, "SVSV"),
-    ("X", 2, "V"), ("Wt", 1, 2), ("Wc", 1, 2, "S"), ("Wt", 1, 3), ("Wc", 1, 3, "S"),
-    ("M1", 2, 1), ("E1", 2, 1, "SVSV"), ("qX", 2), ("Wq", 1, 2), ("Wq", 1, 3),
-    ("M1", 0, 2), ("E1", 0, 2, "SVSV"), ("X", 3, "V"), ("Wt", 2, 2), ("Wc", 2, 2, "S"),
-    ("Wt", 2, 3), ("Wc", 2, 3, "S"), ("M1", 1, 2), ("E1", 1, 2, "SVSV"), ("qX", 3),
-    ("Wq", 2, 2), ("Wq", 2, 3), ("M1", 2, 2), ("E1", 2, 2, "SVSV"), ("M1", 0, 3),
-    ("E1", 0, 3, "SVSV"), ("M0", 1, 0), ("E0", 1, 0, "SVSV"), ("M1", 1, 3), ("E1", 1, 3, "SVSV"),
-    ("M0", 1, 1), ("E0", 1, 1, "SVSV"), ("M1", 2, 3), ("E1", 2, 3, "SVSV"),
+    ("Z", 8, "g"), ("Wt", 0, 0), ("Z", 2, "n"), ("Wc", 0, 0, "S"), ("Wt", 0, 1),
+    ("Wc", 0, 1, "S"), ("SH",), ("Ft", 0), ("Ft", 2), ("Z", 2, "n"),
+    ("D", 0, "V"), ("Fc", 0), ("Fc", 4), ("Fc", 2), ("Wt", 1, 0),
+    ("Z", 2, "n"), ("Wc", 1, 0, "S"), ("Wt", 1, 1), ("Z", 2, "n"), ("Wc", 1, 1, "S"),
+    ("Wq", 0, 0), ("Wq", 0, 1), ("qF",), ("Wt", 2, 0), ("Z", 2, "n"),
+    ("Wc", 2, 0, "S"), ("Wt", 2, 1), ("Wc", 2, 1, "S"), ("Wq", 1, 0), ("Wq", 1, 1),
+    ("Wq", 2, 0), ("Wq", 2, 1), ("M0", 0, 0), ("qD", 0), ("E0", 0, 0, "SSSS"),
+    ("X", 0, "V"), ("D", 1, "V"), ("qX", 0), ("M0", 0, 1), ("D", 2, "V"),
+    ("E0", 0, 1, "SSSS"), ("qD", 1), ("qD", 2), ("M1", 0, 0), ("E1", 0, 0, "SSVS"),
+    ("X", 1, "V"), ("M1", 1, 0), ("E1", 1, 0, "SVSS"), ("qX", 1), ("Wt", 0, 2),
+    ("Wc", 0, 2, "S"), ("M1", 2, 0), ("E1", 2, 0, "SVSV"), ("Wt", 0, 3), ("Wc", 0, 3, "S"),
+    ("M1", 0, 1), ("E1", 0, 1, "SVSV"), ("Wq", 0, 2), ("Wq", 0, 3), ("Wt", 1, 2),
+    ("Wc", 1, 2, "S"), ("M1", 1, 1), ("E1", 1, 1, "SVSV"), ("X", 2, "V"), ("Wt", 1, 3),
+    ("Wc", 1, 3, "S"), ("M1", 2, 1), ("E1", 2, 1, "SVSV"), ("qX", 2), ("Wq", 1, 2),
+    ("Wq", 1, 3), ("Wt", 2, 2), ("Wc", 2, 2, "S"), ("M1", 0, 2), ("E1", 0, 2, "SVSV"),
+    ("X", 3, "V"), ("Wt", 2, 3), ("Wc", 2, 3, "S"), ("M1", 1, 2), ("E1", 1, 2, "SVSV"),
+    ("qX", 3), ("Wq", 2, 2), ("Wq", 2, 3), ("M1", 2, 2), ("E1", 2, 2, "SVSV"),
+    ("M1", 0, 3), ("E1", 0, 3, "SVSV"), ("M0", 1, 0), ("E0", 1, 0, "SVSV"), ("M1", 1, 3),
+    ("E1", 1, 3, "SVSV"), ("M0", 1, 1), ("E0", 1, 1, "SVSV"), ("M1", 2, 3), ("E1", 2, 3, "SVSV"),
 )
 
 
@@ -101,6 +102,8 @@ def tile_predictor_pa_v_kernel(tc, x, W1, b1, z, grad_out, out_0, out_1):
         nc.scalar.activation(out=warm[:], in_=warm[:], func=ACT.Tanh)
         ident = const.tile([P, P], F32, name="ident")
         make_identity(nc, ident[:])
+        zeros = const.tile([P, C], BF16, name="zeros")
+        nc.vector.memset(zeros[:], 0.0)
         shift_b = const.tile([P, P], BF16, name="shift_b")
         nc.vector.memset(shift_b[:], 0.0)
         nc.vector.tensor_copy(out=shift_b[:, 0 : P - 1], in_=ident[:, 1:P])
@@ -147,6 +150,12 @@ def tile_predictor_pa_v_kernel(tc, x, W1, b1, z, grad_out, out_0, out_1):
 
         banks = {}
         groups = {}
+
+        def warm_pe(n, src):
+            w = acc.tile([P, C], F32, name="acc", tag="acc")
+            rhs = {"c": zeros[:], "g": g_sb[:, 0, :], "n": ng[:, 0, :]}[src]
+            for i in range(n):
+                nc.tensor.matmul(out=w[:], lhsT=shift_b[:], rhs=rhs, start=True, stop=True)
 
         def shift_rows():
             sh = tp.tile([P, 2 * C], BF16, name="sh", tag="tp")
@@ -282,6 +291,8 @@ def tile_predictor_pa_v_kernel(tc, x, W1, b1, z, grad_out, out_0, out_1):
             kind = step[0]
             if kind == "SH":
                 shift_rows()
+            elif kind == "Z":
+                warm_pe(step[1], step[2])
             elif kind == "Ft":
                 f_transpose(step[1])
             elif kind == "Fc":

@@ -18,30 +18,35 @@ ALU = mybir.AluOpType
 P = 128
 
 LOADS = (
-    ("g",), ("z", 0), ("z", 1), ("w", 0, 0), ("w", 1, 0),
-    ("w", 2, 0), ("x", 0), ("x", 1), ("w", 0, 1), ("w", 1, 1),
-    ("w", 2, 1),
+    ("g",), ("z", 0), ("z", 1), ("w", 0, 0, 2),
+    ("w", 1, 0, 2), ("w", 2, 0, 2), ("x", 0, 4), ("w", 0, 2, 2),
+    ("w", 1, 2, 2), ("w", 2, 2, 2),
 )
 PLAN = (
-    ("Z", 8, "g"), ("Wt", 0, 0), ("Z", 2, "n"), ("Wc", 0, 0, "S"), ("Wt", 0, 1),
-    ("Wc", 0, 1, "S"), ("SH",), ("Ft", 0), ("Ft", 2), ("Z", 2, "n"),
-    ("D", 0, "V"), ("Fc", 0), ("Fc", 4), ("Fc", 2), ("Wt", 1, 0),
-    ("Z", 2, "n"), ("Wc", 1, 0, "S"), ("Wt", 1, 1), ("Z", 2, "n"), ("Wc", 1, 1, "S"),
-    ("Wq", 0, 0), ("Wq", 0, 1), ("qF",), ("Wt", 2, 0), ("Z", 2, "n"),
-    ("Wc", 2, 0, "S"), ("Wt", 2, 1), ("Wc", 2, 1, "S"), ("Wq", 1, 0), ("Wq", 1, 1),
-    ("Wq", 2, 0), ("Wq", 2, 1), ("M0", 0, 0), ("qD", 0), ("E0", 0, 0, "SSSS"),
-    ("X", 0, "V"), ("D", 1, "V"), ("qX", 0), ("M0", 0, 1), ("D", 2, "V"),
-    ("E0", 0, 1, "SSSS"), ("qD", 1), ("qD", 2), ("M1", 0, 0), ("E1", 0, 0, "SSVS"),
-    ("X", 1, "V"), ("M1", 1, 0), ("E1", 1, 0, "SVSS"), ("qX", 1), ("Wt", 0, 2),
-    ("Wc", 0, 2, "S"), ("M1", 2, 0), ("E1", 2, 0, "SVSV"), ("Wt", 0, 3), ("Wc", 0, 3, "S"),
-    ("M1", 0, 1), ("E1", 0, 1, "SVSV"), ("Wq", 0, 2), ("Wq", 0, 3), ("Wt", 1, 2),
-    ("Wc", 1, 2, "S"), ("M1", 1, 1), ("E1", 1, 1, "SVSV"), ("X", 2, "V"), ("Wt", 1, 3),
-    ("Wc", 1, 3, "S"), ("M1", 2, 1), ("E1", 2, 1, "SVSV"), ("qX", 2), ("Wq", 1, 2),
-    ("Wq", 1, 3), ("Wt", 2, 2), ("Wc", 2, 2, "S"), ("M1", 0, 2), ("E1", 0, 2, "SVSV"),
-    ("X", 3, "V"), ("Wt", 2, 3), ("Wc", 2, 3, "S"), ("M1", 1, 2), ("E1", 1, 2, "SVSV"),
-    ("qX", 3), ("Wq", 2, 2), ("Wq", 2, 3), ("M1", 2, 2), ("E1", 2, 2, "SVSV"),
-    ("M1", 0, 3), ("E1", 0, 3, "SVSV"), ("M0", 1, 0), ("E0", 1, 0, "SVSV"), ("M1", 1, 3),
-    ("E1", 1, 3, "SVSV"), ("M0", 1, 1), ("E0", 1, 1, "SVSV"), ("M1", 2, 3), ("E1", 2, 3, "SVSV"),
+    ("Z", 8, "g"), ("Wt", 0, 0), ("Z", 2, "n"), ("Wc", 0, 0, "S"),
+    ("Wt", 0, 1), ("Wc", 0, 1, "S"), ("SH",), ("Ft", 0),
+    ("Ft", 2), ("Z", 2, "n"), ("D", 0, "V"), ("Fc", 0),
+    ("Fc", 4), ("Fc", 2), ("Wt", 1, 0), ("Z", 2, "n"),
+    ("Wc", 1, 0, "S"), ("Wt", 1, 1), ("Z", 2, "n"), ("Wc", 1, 1, "S"),
+    ("Wq", 0, 0), ("Wq", 0, 1), ("qF",), ("Wt", 2, 0),
+    ("Z", 2, "n"), ("Wc", 2, 0, "S"), ("Wt", 2, 1), ("Wc", 2, 1, "S"),
+    ("Wq", 1, 0), ("Wq", 1, 1), ("Wq", 2, 0), ("Wq", 2, 1),
+    ("M0", 0, 0), ("qD", 0), ("E0", 0, 0, "SSSS", False), ("X", 0, "V"),
+    ("D", 1, "V"), ("qX", 0), ("M0", 0, 1), ("D", 2, "V"),
+    ("E0", 0, 1, "SSSS", False), ("qD", 1), ("qD", 2), ("M1", 0, 0),
+    ("E1", 0, 0, "SSVS", False), ("X", 1, "V"), ("M1", 1, 0), ("E1", 1, 0, "SVSS", False),
+    ("qX", 1), ("Wt", 0, 2), ("Wc", 0, 2, "S"), ("M1", 2, 0),
+    ("E1", 2, 0, "SVSV", False), ("Wt", 0, 3), ("Wc", 0, 3, "S"), ("M1", 0, 1),
+    ("E1", 0, 1, "SVSV", False), ("Wq", 0, 2), ("Wq", 0, 3), ("Wt", 1, 2),
+    ("Wc", 1, 2, "S"), ("M1", 1, 1), ("E1", 1, 1, "SVSV", False), ("X", 2, "V"),
+    ("Wt", 1, 3), ("Wc", 1, 3, "S"), ("M1", 2, 1), ("E1", 2, 1, "SVSV", False),
+    ("qX", 2), ("Wq", 1, 2), ("Wq", 1, 3), ("Wt", 2, 2),
+    ("Wc", 2, 2, "S"), ("M1", 0, 2), ("E1", 0, 2, "SVSV", False), ("X", 3, "V"),
+    ("Wt", 2, 3), ("Wc", 2, 3, "S"), ("M1", 1, 2), ("E1", 1, 2, "SVSV", False),
+    ("qX", 3), ("Wq", 2, 2), ("Wq", 2, 3), ("M1", 2, 2),
+    ("E1", 2, 2, "SVSV", False), ("M1", 0, 3), ("E1", 0, 3, "SVSV", False), ("M1", 1, 3),
+    ("E1", 1, 3, "SVSV", False), ("M1", 2, 3), ("E1", 2, 3, "SVSV", False), ("M0", 1, 0),
+    ("E0", 1, 0, "SVSV", True), ("M0", 1, 1), ("E0", 1, 1, "SVSV", True),
 )
 
 
@@ -54,8 +59,8 @@ def tile_predictor_pa_v_kernel(tc, x, W1, b1, z, grad_out, out_0, out_1):
         keep = ctx.enter_context(tc.tile_pool(name="keep", bufs=1))
         grp = ctx.enter_context(tc.tile_pool(name="grp", bufs=5))
         stage = ctx.enter_context(tc.tile_pool(name="stage", bufs=6))
-        tp = ctx.enter_context(tc.psum_pool(name="tp", bufs=4))
-        acc = ctx.enter_context(tc.psum_pool(name="acc", bufs=4))
+        tp = ctx.enter_context(tc.psum_pool(name="tp", bufs=3))
+        acc = ctx.enter_context(tc.psum_pool(name="acc", bufs=5))
 
         engines = {"S": nc.scalar.copy, "V": nc.vector.tensor_copy}
 
@@ -74,18 +79,20 @@ def tile_predictor_pa_v_kernel(tc, x, W1, b1, z, grad_out, out_0, out_1):
             nc.sync.dma_start(out=zt[:], in_=z_view[:, 2 * i : 2 * i + 2, :])
             z_sb[i] = zt
 
-        def load_x(h):
-            xt = keep.tile([P, 4, 1024], BF16, name="x%d" % h)
-            nc.sync.dma_start(out=xt[:], in_=x_view[:, :, 1024 * h : 1024 * (h + 1)])
-            x_sb[h] = xt
+        def load_x(b, n):
+            xt = keep.tile([P, 4, 512 * n], BF16, name="x%d" % b)
+            nc.sync.dma_start(out=xt[:], in_=x_view[:, :, 512 * b : 512 * (b + n)])
+            for i in range(n):
+                x_sb[b + i] = xt[:, :, 512 * i : 512 * (i + 1)]
 
-        def load_w(k, h):
-            wt = keep.tile([P, 2, 4, C], BF16, name="w%d%d" % (k, h))
+        def load_w(k, bb, n):
+            wt = keep.tile([P, n, 4, C], BF16, name="w%d%d" % (k, bb))
             nc.sync.dma_start(
                 out=wt[:],
-                in_=W1[k, 1024 * h : 1024 * (h + 1), :].rearrange("(b m t) c -> m b t c", b=2, t=4),
+                in_=W1[k, 512 * bb : 512 * (bb + n), :].rearrange("(b m t) c -> m b t c", b=n, t=4),
             )
-            w_sb[(k, h)] = wt
+            for i in range(n):
+                w_sb[(k, bb + i)] = wt[:, i, :, :]
 
         for step in LOADS:
             if step[0] == "g":
@@ -93,9 +100,9 @@ def tile_predictor_pa_v_kernel(tc, x, W1, b1, z, grad_out, out_0, out_1):
             elif step[0] == "z":
                 load_z(step[1])
             elif step[0] == "x":
-                load_x(step[1])
+                load_x(step[1], step[2])
             else:
-                load_w(step[1], step[2])
+                load_w(step[1], step[2], step[3])
 
         warm = const.tile([P, 8], F32, name="warm")
         nc.vector.memset(warm[:], 0.0)
@@ -195,7 +202,7 @@ def tile_predictor_pa_v_kernel(tc, x, W1, b1, z, grad_out, out_0, out_1):
 
         def x_group(b, eng):
             g = grp.tile([P, 4 * 512], BF16, name="gx", tag="grp", align_bytes=64)
-            src = x_sb[b // 2][:, :, 512 * (b % 2) : 512 * (b % 2 + 1)]
+            src = x_sb[b]
             engines[eng](
                 out=g[:].rearrange("p (t m j) -> p t m j", t=4, j=4),
                 in_=src.rearrange("p j (m t) -> p t m j", t=4),
@@ -211,7 +218,7 @@ def tile_predictor_pa_v_kernel(tc, x, W1, b1, z, grad_out, out_0, out_1):
             for half in range(2):
                 bank = tp.tile([P, 4 * P], F32, name="wt", tag="tp")
                 for tl in range(2):
-                    words = w_sb[(k, bb // 2)][:, bb % 2, 2 * half + tl, :].bitcast(F32)
+                    words = w_sb[(k, bb)][:, 2 * half + tl, :].bitcast(F32)
                     for u in range(2):
                         q = 2 * tl + u
                         nc.tensor.transpose(bank[:, P * q : P * (q + 1)], words[:, u : C // 2 : 2], ident[:])
@@ -249,13 +256,16 @@ def tile_predictor_pa_v_kernel(tc, x, W1, b1, z, grad_out, out_0, out_1):
                 accs.append(a)
             banks[("O1", k, b)] = accs
 
-        def out1_store(k, b, pattern):
+        def out1_store(k, b, pattern, fine):
             st = stage.tile([P, 4, C], F32, name="st", tag="st")
             accs = banks[("O1", k, b)]
             dst = out_1[k, 512 * b : 512 * (b + 1), :].rearrange("(m t) c -> m t c", t=4)
             for t in range(4):
                 engines[pattern[t]](out=st[:, t, :], in_=accs[t][:])
-            nc.sync.dma_start(out=dst, in_=st[:])
+                if fine:
+                    nc.sync.dma_start(out=dst[:, t, :], in_=st[:, t, :])
+            if not fine:
+                nc.sync.dma_start(out=dst, in_=st[:])
 
         out_0_view = out_0.rearrange("(n j) e -> n j e", j=4)
 
@@ -280,12 +290,19 @@ def tile_predictor_pa_v_kernel(tc, x, W1, b1, z, grad_out, out_0, out_1):
                 accs.append(a)
             banks[("O0", h, jp)] = accs
 
-        def out0_store(h, jp, pattern):
+        def out0_store(h, jp, pattern, fine):
             st = stage.tile([P, 2, 1024], F32, name="st", tag="st")
             accs = banks[("O0", h, jp)]
             for q in range(4):
-                engines[pattern[q]](out=st[:, q // 2, 512 * (q % 2) : 512 * (q % 2 + 1)], in_=accs[q][:])
-            nc.sync.dma_start(out=out_0_view[:, 2 * jp : 2 * jp + 2, 1024 * h : 1024 * (h + 1)], in_=st[:])
+                cols = slice(512 * (q % 2), 512 * (q % 2 + 1))
+                engines[pattern[q]](out=st[:, q // 2, cols], in_=accs[q][:])
+                if fine:
+                    nc.sync.dma_start(
+                        out=out_0_view[:, 2 * jp + q // 2, 1024 * h + 512 * (q % 2) : 1024 * h + 512 * (q % 2 + 1)],
+                        in_=st[:, q // 2, cols],
+                    )
+            if not fine:
+                nc.sync.dma_start(out=out_0_view[:, 2 * jp : 2 * jp + 2, 1024 * h : 1024 * (h + 1)], in_=st[:])
 
         for step in PLAN:
             kind = step[0]
@@ -316,10 +333,10 @@ def tile_predictor_pa_v_kernel(tc, x, W1, b1, z, grad_out, out_0, out_1):
             elif kind == "M1":
                 out1_mm(step[1], step[2])
             elif kind == "E1":
-                out1_store(step[1], step[2], step[3])
+                out1_store(step[1], step[2], step[3], step[4])
             elif kind == "M0":
                 out0_mm(step[1], step[2])
             elif kind == "E0":
-                out0_store(step[1], step[2], step[3])
+                out0_store(step[1], step[2], step[3], step[4])
             else:
                 raise ValueError(kind)

@@ -3,8 +3,8 @@ from contextlib import ExitStack
 import concourse.mybir as mybir
 from concourse.masks import make_identity
 
-N_TOK, E, C, TAPS = 512, 2048, 512, 3
-FLOPS = 2 * 2 * TAPS * N_TOK * E * C
+TOKENS, E, C, TAPS = 512, 2048, 512, 3
+FLOPS = 2 * 2 * TAPS * TOKENS * E * C
 
 F32 = mybir.dt.float32
 BF16 = mybir.dt.bfloat16
@@ -16,38 +16,10 @@ ACT = mybir.ActivationFunctionType
 ALU = mybir.AluOpType
 
 P = 128
-
-LOADS = (
-    ("g",), ("z", 0), ("z", 1), ("w", 0, 0, 2),
-    ("w", 1, 0, 2), ("w", 2, 0, 2), ("x", 0, 4), ("w", 0, 2, 2),
-    ("w", 1, 2, 2), ("w", 2, 2, 2),
-)
-PLAN = (
-    ("Z", 8, "g"), ("Wt", 0, 0), ("Z", 2, "n"), ("Wc", 0, 0, "S"),
-    ("Wt", 0, 1), ("Wc", 0, 1, "S"), ("SH",), ("Ft", 0),
-    ("Ft", 2), ("Z", 2, "n"), ("D", 0, "V"), ("Fc", 0),
-    ("Fc", 4), ("Fc", 2), ("Wt", 1, 0), ("Z", 2, "n"),
-    ("Wc", 1, 0, "S"), ("Wt", 1, 1), ("Z", 2, "n"), ("Wc", 1, 1, "S"),
-    ("Wq", 0, 0), ("Wq", 0, 1), ("qF",), ("Wt", 2, 0),
-    ("Z", 2, "n"), ("Wc", 2, 0, "S"), ("Wt", 2, 1), ("Wc", 2, 1, "S"),
-    ("Wq", 1, 0), ("Wq", 1, 1), ("Wq", 2, 0), ("Wq", 2, 1),
-    ("M0", 0, 0), ("qD", 0), ("E0", 0, 0, "SSSS", False), ("X", 0, "V"),
-    ("D", 1, "V"), ("qX", 0), ("M0", 0, 1), ("D", 2, "V"),
-    ("E0", 0, 1, "SSSS", False), ("qD", 1), ("qD", 2), ("M1", 0, 0),
-    ("E1", 0, 0, "SSVS", False), ("X", 1, "V"), ("M1", 1, 0), ("E1", 1, 0, "SVSS", False),
-    ("qX", 1), ("Wt", 0, 2), ("Wc", 0, 2, "S"), ("M1", 2, 0),
-    ("E1", 2, 0, "SVSV", False), ("Wt", 0, 3), ("Wc", 0, 3, "S"), ("M1", 0, 1),
-    ("E1", 0, 1, "SVSV", False), ("Wq", 0, 2), ("Wq", 0, 3), ("Wt", 1, 2),
-    ("Wc", 1, 2, "S"), ("M1", 1, 1), ("E1", 1, 1, "SVSV", False), ("X", 2, "V"),
-    ("Wt", 1, 3), ("Wc", 1, 3, "S"), ("M1", 2, 1), ("E1", 2, 1, "SVSV", False),
-    ("qX", 2), ("Wq", 1, 2), ("Wq", 1, 3), ("Wt", 2, 2),
-    ("Wc", 2, 2, "S"), ("M1", 0, 2), ("E1", 0, 2, "SVSV", False), ("X", 3, "V"),
-    ("Wt", 2, 3), ("Wc", 2, 3, "S"), ("M1", 1, 2), ("E1", 1, 2, "SVSV", False),
-    ("qX", 3), ("Wq", 2, 2), ("Wq", 2, 3), ("M1", 2, 2),
-    ("E1", 2, 2, "SVSV", False), ("M1", 0, 3), ("E1", 0, 3, "SVSV", False), ("M1", 1, 3),
-    ("E1", 1, 3, "SVSV", False), ("M1", 2, 3), ("E1", 2, 3, "SVSV", False), ("M0", 1, 0),
-    ("E0", 1, 0, "SVSV", True), ("M0", 1, 1), ("E0", 1, 1, "SVSV", True),
-)
+PACK = 4
+PANEL = 512
+PANELS = E // PANEL
+SLOTS = PACK + TAPS - 1
 
 
 def tile_predictor_pa_v_kernel(tc, x, W1, b1, z, grad_out, out_0, out_1):
@@ -57,286 +29,273 @@ def tile_predictor_pa_v_kernel(tc, x, W1, b1, z, grad_out, out_0, out_1):
         const = ctx.enter_context(tc.tile_pool(name="const", bufs=1))
         head = ctx.enter_context(tc.tile_pool(name="head", bufs=1))
         keep = ctx.enter_context(tc.tile_pool(name="keep", bufs=1))
-        grp = ctx.enter_context(tc.tile_pool(name="grp", bufs=5))
-        stage = ctx.enter_context(tc.tile_pool(name="stage", bufs=6))
-        tp = ctx.enter_context(tc.psum_pool(name="tp", bufs=3))
-        acc = ctx.enter_context(tc.psum_pool(name="acc", bufs=5))
+        grouped = ctx.enter_context(tc.tile_pool(name="grouped", bufs=5))
+        staged = ctx.enter_context(tc.tile_pool(name="staged", bufs=6))
+        turned = ctx.enter_context(tc.psum_pool(name="turned", bufs=4))
+        product = ctx.enter_context(tc.psum_pool(name="product", bufs=4))
 
-        engines = {"S": nc.scalar.copy, "V": nc.vector.tensor_copy}
+        copy_on = {"S": nc.scalar.copy, "V": nc.vector.tensor_copy}
 
-        g_sb = head.tile([P, 4, C], BF16, name="g_sb")
-        z_view = z.rearrange("(p j) c -> p j c", j=4)
-        x_view = x.rearrange("(p j) e -> p j e", j=4)
-        z_sb = {}
-        x_sb = {}
+        g_sb = head.tile([P, PACK, C], BF16, name="g_sb")
+        nc.sync.dma_start(out=g_sb[:], in_=grad_out.rearrange("(p j) c -> p j c", j=PACK))
+        z_view = z.rearrange("(p j) c -> p j c", j=PACK)
+        z_sb = []
+        for i in range(2):
+            z_half = head.tile([P, 2, C], F32, name="z%d" % i)
+            nc.sync.dma_start(out=z_half[:], in_=z_view[:, 2 * i : 2 * i + 2, :])
+            z_sb.append(z_half)
+
         w_sb = {}
 
-        def load_g():
-            nc.sync.dma_start(out=g_sb[:], in_=grad_out.rearrange("(p j) c -> p j c", j=4))
+        def load_w(k, h):
+            pair = keep.tile([P, 2, PACK, C], BF16, name="w%d%d" % (k, h))
+            rows = W1[k, 2 * PANEL * h : 2 * PANEL * (h + 1), :]
+            nc.sync.dma_start(out=pair[:], in_=rows.rearrange("(b m t) c -> m b t c", b=2, t=PACK))
+            for i in range(2):
+                w_sb[(k, 2 * h + i)] = pair[:, i, :, :]
 
-        def load_z(i):
-            zt = head.tile([P, 2, C], F32, name="z%d" % i)
-            nc.sync.dma_start(out=zt[:], in_=z_view[:, 2 * i : 2 * i + 2, :])
-            z_sb[i] = zt
+        for k in range(TAPS):
+            load_w(k, 0)
+        x_sb = keep.tile([P, PACK, E], BF16, name="x_sb")
+        nc.sync.dma_start(out=x_sb[:], in_=x.rearrange("(p j) e -> p j e", j=PACK))
+        for k in range(TAPS):
+            load_w(k, 1)
 
-        def load_x(b, n):
-            xt = keep.tile([P, 4, 512 * n], BF16, name="x%d" % b)
-            nc.sync.dma_start(out=xt[:], in_=x_view[:, :, 512 * b : 512 * (b + n)])
-            for i in range(n):
-                x_sb[b + i] = xt[:, :, 512 * i : 512 * (i + 1)]
-
-        def load_w(k, bb, n):
-            wt = keep.tile([P, n, 4, C], BF16, name="w%d%d" % (k, bb))
-            nc.sync.dma_start(
-                out=wt[:],
-                in_=W1[k, 512 * bb : 512 * (bb + n), :].rearrange("(b m t) c -> m b t c", b=n, t=4),
-            )
-            for i in range(n):
-                w_sb[(k, bb + i)] = wt[:, i, :, :]
-
-        for step in LOADS:
-            if step[0] == "g":
-                load_g()
-            elif step[0] == "z":
-                load_z(step[1])
-            elif step[0] == "x":
-                load_x(step[1], step[2])
-            else:
-                load_w(step[1], step[2], step[3])
-
-        warm = const.tile([P, 8], F32, name="warm")
-        nc.vector.memset(warm[:], 0.0)
-        nc.scalar.activation(out=warm[:], in_=warm[:], func=ACT.Tanh)
+        table_warmer = const.tile([P, 8], F32, name="table_warmer")
+        nc.vector.memset(table_warmer[:], 0.0)
+        nc.scalar.activation(out=table_warmer[:], in_=table_warmer[:], func=ACT.Tanh)
         ident = const.tile([P, P], F32, name="ident")
         make_identity(nc, ident[:])
-        zeros = const.tile([P, C], BF16, name="zeros")
-        nc.vector.memset(zeros[:], 0.0)
-        shift_b = const.tile([P, P], BF16, name="shift_b")
-        nc.vector.memset(shift_b[:], 0.0)
-        nc.vector.tensor_copy(out=shift_b[:, 0 : P - 1], in_=ident[:, 1:P])
+        shift = const.tile([P, P], BF16, name="shift")
+        nc.vector.memset(shift[:], 0.0)
+        nc.vector.tensor_copy(out=shift[:, 0 : P - 1], in_=ident[:, 1:P])
 
-        dzb = keep.tile([P, 6, C], BF16, name="dzb")
-        ng = head.tile([P, 4, C], BF16, name="ng")
-        nc.gpsimd.tensor_scalar(out=ng[:], in0=g_sb[:], scalar1=-1.0, scalar2=0.0, op0=ALU.mult, op1=ALU.add)
+        dz = keep.tile([P, SLOTS, C], BF16, name="dz")
+        neg_g = head.tile([P, PACK, C], BF16, name="neg_g")
+        nc.gpsimd.tensor_scalar(out=neg_g[:], in0=g_sb[:], scalar1=-1.0, scalar2=0.0, op0=ALU.mult, op1=ALU.add)
         th = []
         for i in range(2):
-            tt = head.tile([P, 2, C], F32, name="th%d" % i)
-            nc.scalar.activation(out=tt[:], in_=z_sb[i][:], func=ACT.Tanh)
-            th.append(tt)
+            th_half = head.tile([P, 2, C], F32, name="th%d" % i)
+            nc.scalar.activation(out=th_half[:], in_=z_sb[i][:], func=ACT.Tanh)
+            th.append(th_half)
         nc.vector.tensor_tensor(out=th[0][:], in0=th[0][:], in1=th[0][:], op=ALU.mult)
         nc.scalar.activation(out=th[1][:], in_=th[1][:], func=ACT.Square)
         for i in range(2):
             nc.vector.scalar_tensor_tensor(
-                out=dzb[:, 2 * i : 2 * i + 2, :],
+                out=dz[:, 2 * i : 2 * i + 2, :],
                 in0=th[i][:],
                 scalar=1.0,
-                in1=ng[:, 2 * i : 2 * i + 2, :],
+                in1=neg_g[:, 2 * i : 2 * i + 2, :],
                 op0=ALU.subtract,
                 op1=ALU.mult,
             )
 
-        xq = keep.tile([P, E], U32, name="xq", align_bytes=64)
-        xs = keep.tile([P, E], U8, name="xs", align_bytes=64)
-        wq = []
-        ws = []
-        dq = []
-        ds = []
+        x_codes = keep.tile([P, E], U32, name="x_codes", align_bytes=64)
+        x_scales = keep.tile([P, E], U8, name="x_scales", align_bytes=64)
+        w_codes = []
+        w_scales = []
+        d_codes = []
+        d_scales = []
         for k in range(TAPS):
-            wqk = keep.tile([P, E], U32, name="wq%d" % k, align_bytes=64)
-            wsk = keep.tile([P, E], U8, name="ws%d" % k, align_bytes=64)
-            dqk = keep.tile([P, C], U32, name="dq%d" % k, align_bytes=64)
-            dsk = keep.tile([P, C], U8, name="ds%d" % k, align_bytes=64)
-            wq.append(wqk)
-            ws.append(wsk)
-            dq.append(dqk)
-            ds.append(dsk)
-        fq = keep.tile([P, 6 * P], U32, name="fq", align_bytes=64)
-        fs = keep.tile([P, 6 * P], U8, name="fs", align_bytes=64)
-        gf = keep.tile([P, 6 * P * 4], BF16, name="gf", align_bytes=64)
-        gf_words = gf[:].bitcast(F32).rearrange("p (s n u) -> p s n u", s=6, u=2)
+            wc = keep.tile([P, E], U32, name="w_codes%d" % k, align_bytes=64)
+            wsc = keep.tile([P, E], U8, name="w_scales%d" % k, align_bytes=64)
+            dc = keep.tile([P, C], U32, name="d_codes%d" % k, align_bytes=64)
+            dsc = keep.tile([P, C], U8, name="d_scales%d" % k, align_bytes=64)
+            w_codes.append(wc)
+            w_scales.append(wsc)
+            d_codes.append(dc)
+            d_scales.append(dsc)
+        t_codes = keep.tile([P, SLOTS * P], U32, name="t_codes", align_bytes=64)
+        t_scales = keep.tile([P, SLOTS * P], U8, name="t_scales", align_bytes=64)
+        t_grouped = keep.tile([P, SLOTS * P * PACK], BF16, name="t_grouped", align_bytes=64)
+        t_words = t_grouped[:].bitcast(F32).rearrange("p (s n u) -> p s n u", s=SLOTS, u=2)
+        nc.vector.memset(t_grouped[:].rearrange("p (s n t) -> p s n t", s=SLOTS, t=PACK)[:, PACK:SLOTS, P - 1, :], 0.0)
 
         banks = {}
-        groups = {}
+        tiles = {}
 
-        def warm_pe(n, src):
-            w = acc.tile([P, C], F32, name="acc", tag="acc")
-            rhs = {"c": zeros[:], "g": g_sb[:, 0, :], "n": ng[:, 0, :]}[src]
-            for i in range(n):
-                nc.tensor.matmul(out=w[:], lhsT=shift_b[:], rhs=rhs, start=True, stop=True)
-
-        def shift_rows():
-            sh = tp.tile([P, 2 * C], BF16, name="sh", tag="tp")
+        def shift_tokens():
+            moved = turned.tile([P, 2 * C], BF16, name="moved", tag="bank")
             for j in range(2):
-                nc.tensor.matmul(out=sh[:, C * j : C * (j + 1)], lhsT=shift_b[:], rhs=dzb[:, j, :], start=True, stop=True)
-            nc.scalar.copy(out=dzb[:, 4:6, :], in_=sh[:].rearrange("p (j c) -> p j c", j=2))
+                nc.tensor.matmul(out=moved[:, C * j : C * (j + 1)], lhsT=shift[:], rhs=dz[:, j, :], start=True, stop=True)
+            nc.scalar.copy(out=dz[:, PACK:SLOTS, :], in_=moved[:].rearrange("p (j c) -> p j c", j=2))
 
-        nc.vector.memset(gf[:].rearrange("p (s n t) -> p s n t", s=6, t=4)[:, 4:6, P - 1, :], 0.0)
+        def transpose_rows(bank, q, rows):
+            words = rows.bitcast(F32)
+            for u in range(2):
+                nc.tensor.transpose(bank[:, P * (2 * q + u) : P * (2 * q + u + 1)], words[:, u : C // 2 : 2], ident[:])
 
-        def f_transpose(s0):
-            bank = tp.tile([P, 4 * P], F32, name="ft", tag="tp")
-            for sl in range(2):
-                words = dzb[:, s0 + sl, :].bitcast(F32)
-                for u in range(2):
-                    q = 2 * sl + u
-                    nc.tensor.transpose(bank[:, P * q : P * (q + 1)], words[:, u : C // 2 : 2], ident[:])
-            banks[("F", s0)] = bank
+        def dz_transpose(s0):
+            bank = turned.tile([P, PACK * P], F32, name="dz_t", tag="bank")
+            for i in range(2):
+                transpose_rows(bank, i, dz[:, s0 + i, :])
+            banks[("dz", s0)] = bank
 
-        def f_copy(s0):
-            src = banks[("F", s0 % 4)][:].rearrange("p (s u n) -> p s n u", s=2, u=2)
-            if s0 < 4:
-                nc.vector.tensor_copy(out=gf_words[:, s0 : s0 + 2, :, :], in_=src)
+        def dz_copy(s0):
+            src = banks[("dz", s0 % PACK)][:].rearrange("p (s u n) -> p s n u", s=2, u=2)
+            if s0 < PACK:
+                nc.vector.tensor_copy(out=t_words[:, s0 : s0 + 2, :, :], in_=src)
             else:
-                nc.vector.tensor_copy(out=gf_words[:, s0 : s0 + 2, 0 : P - 1, :], in_=src[:, :, 1:P, :])
+                nc.vector.tensor_copy(out=t_words[:, s0 : s0 + 2, 0 : P - 1, :], in_=src[:, :, 1:P, :])
 
-        def f_quant():
-            nc.vector.quantize_mx(out=fq[:, 0:512].bitcast(E5M2), scales=fs[:, 0:512], in_=gf[:, 0:2048])
-            nc.vector.quantize_mx(out=fq[:, 512:768].bitcast(E5M2), scales=fs[:, 512:768], in_=gf[:, 2048:3072])
-
-        def d_group(k, eng):
-            g = grp.tile([P, 4 * C], BF16, name="gd", tag="grp", align_bytes=64)
-            engines[eng](out=g[:].rearrange("p (c t) -> p c t", t=4), in_=dzb[:, k : k + 4, :].rearrange("p t c -> p c t"))
-            groups[("D", k)] = g
-
-        def d_quant(k):
-            nc.vector.quantize_mx(out=dq[k][:].bitcast(E5M2), scales=ds[k][:], in_=groups[("D", k)][:])
-
-        def x_group(b, eng):
-            g = grp.tile([P, 4 * 512], BF16, name="gx", tag="grp", align_bytes=64)
-            src = x_sb[b]
-            engines[eng](
-                out=g[:].rearrange("p (t m j) -> p t m j", t=4, j=4),
-                in_=src.rearrange("p j (m t) -> p t m j", t=4),
+        def dz_quantize_features():
+            own = PACK * P
+            nc.vector.quantize_mx(
+                out=t_codes[:, 0:own].bitcast(E5M2), scales=t_scales[:, 0:own], in_=t_grouped[:, 0 : PACK * own]
             )
-            groups[("X", b)] = g
+            nc.vector.quantize_mx(
+                out=t_codes[:, own:].bitcast(E5M2), scales=t_scales[:, own:], in_=t_grouped[:, PACK * own :]
+            )
 
-        def x_quant(b):
-            cols = slice(512 * b, 512 * (b + 1))
-            nc.vector.quantize_mx(out=xq[:, cols].bitcast(E4M3), scales=xs[:, cols], in_=groups[("X", b)][:])
+        def d_group(k):
+            g = grouped.tile([P, PACK * C], BF16, name="d_grouped", tag="grouped", align_bytes=64)
+            nc.vector.tensor_copy(
+                out=g[:].rearrange("p (c t) -> p c t", t=PACK), in_=dz[:, k : k + PACK, :].rearrange("p t c -> p c t")
+            )
+            tiles[("d", k)] = g
 
-        def w_transpose(k, bb):
+        def d_quantize(k):
+            nc.vector.quantize_mx(out=d_codes[k][:].bitcast(E5M2), scales=d_scales[k][:], in_=tiles[("d", k)][:])
+
+        def x_group(b):
+            g = grouped.tile([P, PACK * PANEL], BF16, name="x_grouped", tag="grouped", align_bytes=64)
+            nc.vector.tensor_copy(
+                out=g[:].rearrange("p (t m j) -> p t m j", t=PACK, j=PACK),
+                in_=x_sb[:, :, PANEL * b : PANEL * (b + 1)].rearrange("p j (m t) -> p t m j", t=PACK),
+            )
+            tiles[("x", b)] = g
+
+        def x_quantize(b):
+            cols = slice(PANEL * b, PANEL * (b + 1))
+            nc.vector.quantize_mx(out=x_codes[:, cols].bitcast(E4M3), scales=x_scales[:, cols], in_=tiles[("x", b)][:])
+
+        def w_transpose(k, b):
             pair = []
             for half in range(2):
-                bank = tp.tile([P, 4 * P], F32, name="wt", tag="tp")
-                for tl in range(2):
-                    words = w_sb[(k, bb)][:, 2 * half + tl, :].bitcast(F32)
-                    for u in range(2):
-                        q = 2 * tl + u
-                        nc.tensor.transpose(bank[:, P * q : P * (q + 1)], words[:, u : C // 2 : 2], ident[:])
+                bank = turned.tile([P, PACK * P], F32, name="w_t", tag="bank")
+                for i in range(2):
+                    transpose_rows(bank, i, w_sb[(k, b)][:, 2 * half + i, :])
                 pair.append(bank)
-            banks[(k, bb)] = pair
+            banks[("w", k, b)] = pair
 
-        def w_copy(k, bb, eng):
-            g = grp.tile([P, 4 * 512], BF16, name="gw", tag="grp", align_bytes=64)
-            words = g[:].bitcast(F32).rearrange("p (m t u) -> p m t u", t=4, u=2)
+        def w_copy(k, b):
+            g = grouped.tile([P, PACK * PANEL], BF16, name="w_grouped", tag="grouped", align_bytes=64)
+            words = g[:].bitcast(F32).rearrange("p (m t u) -> p m t u", t=PACK, u=2)
             for half in range(2):
-                engines[eng](
+                nc.scalar.copy(
                     out=words[:, :, 2 * half : 2 * half + 2, :],
-                    in_=banks[(k, bb)][half][:].rearrange("p (t u m) -> p m t u", t=2, u=2),
+                    in_=banks[("w", k, b)][half][:].rearrange("p (t u m) -> p m t u", t=2, u=2),
                 )
-            groups[("W", k, bb)] = g
+            tiles[("w", k, b)] = g
 
-        def w_quant(k, bb):
-            cols = slice(512 * bb, 512 * (bb + 1))
-            nc.vector.quantize_mx(out=wq[k][:, cols].bitcast(E4M3), scales=ws[k][:, cols], in_=groups[("W", k, bb)][:])
+        def w_quantize(k, b):
+            cols = slice(PANEL * b, PANEL * (b + 1))
+            nc.vector.quantize_mx(
+                out=w_codes[k][:, cols].bitcast(E4M3), scales=w_scales[k][:, cols], in_=tiles[("w", k, b)][:]
+            )
 
-        def out1_mm(k, b):
-            accs = []
-            for t in range(4):
-                a = acc.tile([P, C], F32, name="acc", tag="acc")
-                cols = slice(512 * b + P * t, 512 * b + P * (t + 1))
+        def out1_unit(k, b, engines):
+            four = []
+            for t in range(PACK):
+                bank = product.tile([P, C], F32, name="bank", tag="bank")
+                cols = slice(PANEL * b + P * t, PANEL * b + P * (t + 1))
                 nc.tensor.matmul_mx(
-                    out=a[:],
-                    lhsT=xq[:, cols].bitcast(E4M3),
-                    lhsT_scale=xs[:, cols],
-                    rhs=dq[k][:].bitcast(E5M2),
-                    rhs_scale=ds[k][:],
+                    out=bank[:],
+                    lhsT=x_codes[:, cols].bitcast(E4M3),
+                    lhsT_scale=x_scales[:, cols],
+                    rhs=d_codes[k][:].bitcast(E5M2),
+                    rhs_scale=d_scales[k][:],
                     start=True,
                     stop=True,
                 )
-                accs.append(a)
-            banks[("O1", k, b)] = accs
+                four.append(bank)
+            st = staged.tile([P, PACK, C], F32, name="st", tag="st")
+            for t in range(PACK):
+                copy_on[engines[t]](out=st[:, t, :], in_=four[t][:])
+            nc.sync.dma_start(
+                out=out_1[k, PANEL * b : PANEL * (b + 1), :].rearrange("(m t) c -> m t c", t=PACK), in_=st[:]
+            )
 
-        def out1_store(k, b, pattern, fine):
-            st = stage.tile([P, 4, C], F32, name="st", tag="st")
-            accs = banks[("O1", k, b)]
-            dst = out_1[k, 512 * b : 512 * (b + 1), :].rearrange("(m t) c -> m t c", t=4)
-            for t in range(4):
-                engines[pattern[t]](out=st[:, t, :], in_=accs[t][:])
-                if fine:
-                    nc.sync.dma_start(out=dst[:, t, :], in_=st[:, t, :])
-            if not fine:
-                nc.sync.dma_start(out=dst, in_=st[:])
+        out_0_view = out_0.rearrange("(n j) e -> n j e", j=PACK)
 
-        out_0_view = out_0.rearrange("(n j) e -> n j e", j=4)
-
-        def out0_mm(h, jp):
-            accs = []
+        def out0_matmuls(h, jp):
+            four = []
             for q in range(4):
                 j = 2 * jp + q // 2
-                bb = 2 * h + q % 2
-                a = acc.tile([P, 512], F32, name="acc", tag="acc")
-                ecols = slice(512 * bb, 512 * (bb + 1))
+                b = 2 * h + q % 2
+                bank = product.tile([P, PANEL], F32, name="bank", tag="bank")
+                e_cols = slice(PANEL * b, PANEL * (b + 1))
                 for k in range(TAPS):
-                    tcols = slice(P * (j + k), P * (j + k + 1))
+                    t_cols = slice(P * (j + k), P * (j + k + 1))
                     nc.tensor.matmul_mx(
-                        out=a[:],
-                        lhsT=fq[:, tcols].bitcast(E5M2),
-                        lhsT_scale=fs[:, tcols],
-                        rhs=wq[k][:, ecols].bitcast(E4M3),
-                        rhs_scale=ws[k][:, ecols],
+                        out=bank[:],
+                        lhsT=t_codes[:, t_cols].bitcast(E5M2),
+                        lhsT_scale=t_scales[:, t_cols],
+                        rhs=w_codes[k][:, e_cols].bitcast(E4M3),
+                        rhs_scale=w_scales[k][:, e_cols],
                         start=(k == 0),
                         stop=(k == TAPS - 1),
                     )
-                accs.append(a)
-            banks[("O0", h, jp)] = accs
+                four.append(bank)
+            banks[("out0", h, jp)] = four
 
-        def out0_store(h, jp, pattern, fine):
-            st = stage.tile([P, 2, 1024], F32, name="st", tag="st")
-            accs = banks[("O0", h, jp)]
+        def out0_store(h, jp, engines):
+            st = staged.tile([P, 2, 2 * PANEL], F32, name="st", tag="st")
             for q in range(4):
-                cols = slice(512 * (q % 2), 512 * (q % 2 + 1))
-                engines[pattern[q]](out=st[:, q // 2, cols], in_=accs[q][:])
-                if fine:
-                    nc.sync.dma_start(
-                        out=out_0_view[:, 2 * jp + q // 2, 1024 * h + 512 * (q % 2) : 1024 * h + 512 * (q % 2 + 1)],
-                        in_=st[:, q // 2, cols],
-                    )
-            if not fine:
-                nc.sync.dma_start(out=out_0_view[:, 2 * jp : 2 * jp + 2, 1024 * h : 1024 * (h + 1)], in_=st[:])
+                copy_on[engines[q]](
+                    out=st[:, q // 2, PANEL * (q % 2) : PANEL * (q % 2 + 1)], in_=banks[("out0", h, jp)][q][:]
+                )
+            nc.sync.dma_start(
+                out=out_0_view[:, 2 * jp : 2 * jp + 2, 2 * PANEL * h : 2 * PANEL * (h + 1)], in_=st[:]
+            )
 
-        for step in PLAN:
-            kind = step[0]
-            if kind == "SH":
-                shift_rows()
-            elif kind == "Z":
-                warm_pe(step[1], step[2])
-            elif kind == "Ft":
-                f_transpose(step[1])
-            elif kind == "Fc":
-                f_copy(step[1])
-            elif kind == "qF":
-                f_quant()
-            elif kind == "D":
-                d_group(step[1], step[2])
-            elif kind == "qD":
-                d_quant(step[1])
-            elif kind == "X":
-                x_group(step[1], step[2])
-            elif kind == "qX":
-                x_quant(step[1])
-            elif kind == "Wt":
-                w_transpose(step[1], step[2])
-            elif kind == "Wc":
-                w_copy(step[1], step[2], step[3])
-            elif kind == "Wq":
-                w_quant(step[1], step[2])
-            elif kind == "M1":
-                out1_mm(step[1], step[2])
-            elif kind == "E1":
-                out1_store(step[1], step[2], step[3], step[4])
-            elif kind == "M0":
-                out0_mm(step[1], step[2])
-            elif kind == "E0":
-                out0_store(step[1], step[2], step[3], step[4])
+        for k in range(TAPS):
+            for b in range(2):
+                w_transpose(k, b)
+                w_copy(k, b)
+            if k == 0:
+                shift_tokens()
+                dz_transpose(0)
+                dz_transpose(2)
+                d_group(0)
+                dz_copy(0)
+                dz_copy(PACK)
+                dz_copy(2)
             else:
-                raise ValueError(kind)
+                w_quantize(k - 1, 0)
+                w_quantize(k - 1, 1)
+            if k == 1:
+                dz_quantize_features()
+        w_quantize(TAPS - 1, 0)
+        w_quantize(TAPS - 1, 1)
+
+        out0_matmuls(0, 0)
+        d_quantize(0)
+        out0_store(0, 0, "SSSS")
+        x_group(0)
+        d_group(1)
+        x_quantize(0)
+        out0_matmuls(0, 1)
+        d_group(2)
+        out0_store(0, 1, "SSSS")
+        d_quantize(1)
+        d_quantize(2)
+
+        late_w = [(k, b) for k in range(TAPS) for b in (2, 3)]
+        for u in range(TAPS * PANELS):
+            b, k = divmod(u, TAPS)
+            if 2 <= u < 2 + len(late_w):
+                w_transpose(*late_w[u - 2])
+                w_copy(*late_w[u - 2])
+            if u >= TAPS * PANELS - 2:
+                jp = u - (TAPS * PANELS - 2)
+                out0_matmuls(1, jp)
+                out0_store(1, jp, "SVSV")
+            out1_unit(k, b, {0: "SSVS", 1: "SVSS"}.get(u, "SVSV"))
+            if k == 0 and b + 1 < PANELS:
+                x_group(b + 1)
+            if 2 <= u < 2 + len(late_w) and u % 2 == 1:
+                w_quantize(*late_w[u - 3])
+                w_quantize(*late_w[u - 2])
+            if k == 1 and b + 1 < PANELS:
+                x_quantize(b + 1)

@@ -20,6 +20,8 @@ PACK = 4
 PANEL = 512
 PANELS = E // PANEL
 SLOTS = PACK + TAPS - 1
+UNITS = TAPS * PANELS
+FIRST_LATE_UNIT = 2
 
 
 def tile_predictor_pa_v_kernel(tc, x, W1, b1, z, grad_out, out_0, out_1):
@@ -50,7 +52,7 @@ def tile_predictor_pa_v_kernel(tc, x, W1, b1, z, grad_out, out_0, out_1):
         def load_w(k, h):
             pair = keep.tile([P, 2, PACK, C], BF16, name="w%d%d" % (k, h))
             rows = W1[k, 2 * PANEL * h : 2 * PANEL * (h + 1), :]
-            nc.sync.dma_start(out=pair[:], in_=rows.rearrange("(b m t) c -> m b t c", b=2, t=PACK))
+            nc.sync.dma_start(out=pair[:], in_=rows.rearrange("(b m r) c -> m b r c", b=2, r=PACK))
             for i in range(2):
                 w_sb[(k, 2 * h + i)] = pair[:, i, :, :]
 
@@ -73,17 +75,17 @@ def tile_predictor_pa_v_kernel(tc, x, W1, b1, z, grad_out, out_0, out_1):
         dz = keep.tile([P, SLOTS, C], BF16, name="dz")
         neg_g = head.tile([P, PACK, C], BF16, name="neg_g")
         nc.gpsimd.tensor_scalar(out=neg_g[:], in0=g_sb[:], scalar1=-1.0, scalar2=0.0, op0=ALU.mult, op1=ALU.add)
-        th = []
+        tanh_sq = []
         for i in range(2):
-            th_half = head.tile([P, 2, C], F32, name="th%d" % i)
-            nc.scalar.activation(out=th_half[:], in_=z_sb[i][:], func=ACT.Tanh)
-            th.append(th_half)
-        nc.vector.tensor_tensor(out=th[0][:], in0=th[0][:], in1=th[0][:], op=ALU.mult)
-        nc.scalar.activation(out=th[1][:], in_=th[1][:], func=ACT.Square)
+            tanh_half = head.tile([P, 2, C], F32, name="tanh%d" % i)
+            nc.scalar.activation(out=tanh_half[:], in_=z_sb[i][:], func=ACT.Tanh)
+            tanh_sq.append(tanh_half)
+        nc.vector.tensor_tensor(out=tanh_sq[0][:], in0=tanh_sq[0][:], in1=tanh_sq[0][:], op=ALU.mult)
+        nc.scalar.activation(out=tanh_sq[1][:], in_=tanh_sq[1][:], func=ACT.Square)
         for i in range(2):
             nc.vector.scalar_tensor_tensor(
                 out=dz[:, 2 * i : 2 * i + 2, :],
-                in0=th[i][:],
+                in0=tanh_sq[i][:],
                 scalar=1.0,
                 in1=neg_g[:, 2 * i : 2 * i + 2, :],
                 op0=ALU.subtract,
@@ -97,22 +99,22 @@ def tile_predictor_pa_v_kernel(tc, x, W1, b1, z, grad_out, out_0, out_1):
         d_codes = []
         d_scales = []
         for k in range(TAPS):
-            wc = keep.tile([P, E], U32, name="w_codes%d" % k, align_bytes=64)
-            wsc = keep.tile([P, E], U8, name="w_scales%d" % k, align_bytes=64)
-            dc = keep.tile([P, C], U32, name="d_codes%d" % k, align_bytes=64)
-            dsc = keep.tile([P, C], U8, name="d_scales%d" % k, align_bytes=64)
-            w_codes.append(wc)
-            w_scales.append(wsc)
-            d_codes.append(dc)
-            d_scales.append(dsc)
+            w_codes_k = keep.tile([P, E], U32, name="w_codes%d" % k, align_bytes=64)
+            w_scales_k = keep.tile([P, E], U8, name="w_scales%d" % k, align_bytes=64)
+            d_codes_k = keep.tile([P, C], U32, name="d_codes%d" % k, align_bytes=64)
+            d_scales_k = keep.tile([P, C], U8, name="d_scales%d" % k, align_bytes=64)
+            w_codes.append(w_codes_k)
+            w_scales.append(w_scales_k)
+            d_codes.append(d_codes_k)
+            d_scales.append(d_scales_k)
         t_codes = keep.tile([P, SLOTS * P], U32, name="t_codes", align_bytes=64)
         t_scales = keep.tile([P, SLOTS * P], U8, name="t_scales", align_bytes=64)
         t_grouped = keep.tile([P, SLOTS * P * PACK], BF16, name="t_grouped", align_bytes=64)
-        t_words = t_grouped[:].bitcast(F32).rearrange("p (s n u) -> p s n u", s=SLOTS, u=2)
+        t_words = t_grouped[:].bitcast(F32).rearrange("p (s n v) -> p s n v", s=SLOTS, v=2)
         nc.vector.memset(t_grouped[:].rearrange("p (s n t) -> p s n t", s=SLOTS, t=PACK)[:, PACK:SLOTS, P - 1, :], 0.0)
 
         banks = {}
-        tiles = {}
+        laid_out = {}
 
         def shift_tokens():
             moved = turned.tile([P, 2 * C], BF16, name="moved", tag="bank")
@@ -120,10 +122,10 @@ def tile_predictor_pa_v_kernel(tc, x, W1, b1, z, grad_out, out_0, out_1):
                 nc.tensor.matmul(out=moved[:, C * j : C * (j + 1)], lhsT=shift[:], rhs=dz[:, j, :], start=True, stop=True)
             nc.scalar.copy(out=dz[:, PACK:SLOTS, :], in_=moved[:].rearrange("p (j c) -> p j c", j=2))
 
-        def transpose_rows(bank, q, rows):
+        def transpose_rows(bank, i, rows):
             words = rows.bitcast(F32)
-            for u in range(2):
-                nc.tensor.transpose(bank[:, P * (2 * q + u) : P * (2 * q + u + 1)], words[:, u : C // 2 : 2], ident[:])
+            for v in range(2):
+                nc.tensor.transpose(bank[:, P * (2 * i + v) : P * (2 * i + v + 1)], words[:, v : C // 2 : 2], ident[:])
 
         def dz_transpose(s0):
             bank = turned.tile([P, PACK * P], F32, name="dz_t", tag="bank")
@@ -132,7 +134,7 @@ def tile_predictor_pa_v_kernel(tc, x, W1, b1, z, grad_out, out_0, out_1):
             banks[("dz", s0)] = bank
 
         def dz_copy(s0):
-            src = banks[("dz", s0 % PACK)][:].rearrange("p (s u n) -> p s n u", s=2, u=2)
+            src = banks[("dz", s0 % PACK)][:].rearrange("p (s v n) -> p s n v", s=2, v=2)
             if s0 < PACK:
                 nc.vector.tensor_copy(out=t_words[:, s0 : s0 + 2, :, :], in_=src)
             else:
@@ -148,26 +150,26 @@ def tile_predictor_pa_v_kernel(tc, x, W1, b1, z, grad_out, out_0, out_1):
             )
 
         def d_group(k):
-            g = grouped.tile([P, PACK * C], BF16, name="d_grouped", tag="grouped", align_bytes=64)
+            laid = grouped.tile([P, PACK * C], BF16, name="d_grouped", tag="grouped", align_bytes=64)
             nc.vector.tensor_copy(
-                out=g[:].rearrange("p (c t) -> p c t", t=PACK), in_=dz[:, k : k + PACK, :].rearrange("p t c -> p c t")
+                out=laid[:].rearrange("p (c t) -> p c t", t=PACK), in_=dz[:, k : k + PACK, :].rearrange("p t c -> p c t")
             )
-            tiles[("d", k)] = g
+            laid_out[("d", k)] = laid
 
         def d_quantize(k):
-            nc.vector.quantize_mx(out=d_codes[k][:].bitcast(E5M2), scales=d_scales[k][:], in_=tiles[("d", k)][:])
+            nc.vector.quantize_mx(out=d_codes[k][:].bitcast(E5M2), scales=d_scales[k][:], in_=laid_out[("d", k)][:])
 
         def x_group(b):
-            g = grouped.tile([P, PACK * PANEL], BF16, name="x_grouped", tag="grouped", align_bytes=64)
+            laid = grouped.tile([P, PACK * PANEL], BF16, name="x_grouped", tag="grouped", align_bytes=64)
             nc.vector.tensor_copy(
-                out=g[:].rearrange("p (t m j) -> p t m j", t=PACK, j=PACK),
-                in_=x_sb[:, :, PANEL * b : PANEL * (b + 1)].rearrange("p j (m t) -> p t m j", t=PACK),
+                out=laid[:].rearrange("p (r m t) -> p r m t", r=PACK, t=PACK),
+                in_=x_sb[:, :, PANEL * b : PANEL * (b + 1)].rearrange("p t (m r) -> p r m t", r=PACK),
             )
-            tiles[("x", b)] = g
+            laid_out[("x", b)] = laid
 
         def x_quantize(b):
             cols = slice(PANEL * b, PANEL * (b + 1))
-            nc.vector.quantize_mx(out=x_codes[:, cols].bitcast(E4M3), scales=x_scales[:, cols], in_=tiles[("x", b)][:])
+            nc.vector.quantize_mx(out=x_codes[:, cols].bitcast(E4M3), scales=x_scales[:, cols], in_=laid_out[("x", b)][:])
 
         def w_transpose(k, b):
             pair = []
@@ -179,26 +181,26 @@ def tile_predictor_pa_v_kernel(tc, x, W1, b1, z, grad_out, out_0, out_1):
             banks[("w", k, b)] = pair
 
         def w_copy(k, b):
-            g = grouped.tile([P, PACK * PANEL], BF16, name="w_grouped", tag="grouped", align_bytes=64)
-            words = g[:].bitcast(F32).rearrange("p (m t u) -> p m t u", t=PACK, u=2)
+            laid = grouped.tile([P, PACK * PANEL], BF16, name="w_grouped", tag="grouped", align_bytes=64)
+            words = laid[:].bitcast(F32).rearrange("p (m r v) -> p m r v", r=PACK, v=2)
             for half in range(2):
                 nc.scalar.copy(
                     out=words[:, :, 2 * half : 2 * half + 2, :],
-                    in_=banks[("w", k, b)][half][:].rearrange("p (t u m) -> p m t u", t=2, u=2),
+                    in_=banks[("w", k, b)][half][:].rearrange("p (r v m) -> p m r v", r=2, v=2),
                 )
-            tiles[("w", k, b)] = g
+            laid_out[("w", k, b)] = laid
 
         def w_quantize(k, b):
             cols = slice(PANEL * b, PANEL * (b + 1))
             nc.vector.quantize_mx(
-                out=w_codes[k][:, cols].bitcast(E4M3), scales=w_scales[k][:, cols], in_=tiles[("w", k, b)][:]
+                out=w_codes[k][:, cols].bitcast(E4M3), scales=w_scales[k][:, cols], in_=laid_out[("w", k, b)][:]
             )
 
         def out1_unit(k, b, engines):
             four = []
-            for t in range(PACK):
+            for r in range(PACK):
                 bank = product.tile([P, C], F32, name="bank", tag="bank")
-                cols = slice(PANEL * b + P * t, PANEL * b + P * (t + 1))
+                cols = slice(PANEL * b + P * r, PANEL * b + P * (r + 1))
                 nc.tensor.matmul_mx(
                     out=bank[:],
                     lhsT=x_codes[:, cols].bitcast(E4M3),
@@ -210,44 +212,42 @@ def tile_predictor_pa_v_kernel(tc, x, W1, b1, z, grad_out, out_0, out_1):
                 )
                 four.append(bank)
             st = staged.tile([P, PACK, C], F32, name="st", tag="st")
-            for t in range(PACK):
-                copy_on[engines[t]](out=st[:, t, :], in_=four[t][:])
+            for r in range(PACK):
+                copy_on[engines[r]](out=st[:, r, :], in_=four[r][:])
             nc.sync.dma_start(
-                out=out_1[k, PANEL * b : PANEL * (b + 1), :].rearrange("(m t) c -> m t c", t=PACK), in_=st[:]
+                out=out_1[k, PANEL * b : PANEL * (b + 1), :].rearrange("(m r) c -> m r c", r=PACK), in_=st[:]
             )
 
         out_0_view = out_0.rearrange("(n j) e -> n j e", j=PACK)
 
-        def out0_matmuls(h, jp):
+        def out0_matmuls(h, j0):
             four = []
-            for q in range(4):
-                j = 2 * jp + q // 2
-                b = 2 * h + q % 2
-                bank = product.tile([P, PANEL], F32, name="bank", tag="bank")
-                e_cols = slice(PANEL * b, PANEL * (b + 1))
-                for k in range(TAPS):
-                    t_cols = slice(P * (j + k), P * (j + k + 1))
-                    nc.tensor.matmul_mx(
-                        out=bank[:],
-                        lhsT=t_codes[:, t_cols].bitcast(E5M2),
-                        lhsT_scale=t_scales[:, t_cols],
-                        rhs=w_codes[k][:, e_cols].bitcast(E4M3),
-                        rhs_scale=w_scales[k][:, e_cols],
-                        start=(k == 0),
-                        stop=(k == TAPS - 1),
-                    )
-                four.append(bank)
-            banks[("out0", h, jp)] = four
+            for j in (j0, j0 + 1):
+                for b in (2 * h, 2 * h + 1):
+                    bank = product.tile([P, PANEL], F32, name="bank", tag="bank")
+                    e_cols = slice(PANEL * b, PANEL * (b + 1))
+                    for k in range(TAPS):
+                        t_cols = slice(P * (j + k), P * (j + k + 1))
+                        nc.tensor.matmul_mx(
+                            out=bank[:],
+                            lhsT=t_codes[:, t_cols].bitcast(E5M2),
+                            lhsT_scale=t_scales[:, t_cols],
+                            rhs=w_codes[k][:, e_cols].bitcast(E4M3),
+                            rhs_scale=w_scales[k][:, e_cols],
+                            start=(k == 0),
+                            stop=(k == TAPS - 1),
+                        )
+                    four.append(bank)
+            banks[("out0", h, j0)] = four
 
-        def out0_store(h, jp, engines):
+        def out0_store(h, j0, engines):
             st = staged.tile([P, 2, 2 * PANEL], F32, name="st", tag="st")
-            for q in range(4):
-                copy_on[engines[q]](
-                    out=st[:, q // 2, PANEL * (q % 2) : PANEL * (q % 2 + 1)], in_=banks[("out0", h, jp)][q][:]
-                )
-            nc.sync.dma_start(
-                out=out_0_view[:, 2 * jp : 2 * jp + 2, 2 * PANEL * h : 2 * PANEL * (h + 1)], in_=st[:]
-            )
+            for i in range(2):
+                for side in range(2):
+                    copy_on[engines[2 * i + side]](
+                        out=st[:, i, PANEL * side : PANEL * (side + 1)], in_=banks[("out0", h, j0)][2 * i + side][:]
+                    )
+                nc.sync.dma_start(out=out_0_view[:, j0 + i, 2 * PANEL * h : 2 * PANEL * (h + 1)], in_=st[:, i, :])
 
         for k in range(TAPS):
             for b in range(2):
@@ -275,27 +275,28 @@ def tile_predictor_pa_v_kernel(tc, x, W1, b1, z, grad_out, out_0, out_1):
         x_group(0)
         d_group(1)
         x_quantize(0)
-        out0_matmuls(0, 1)
+        out0_matmuls(0, 2)
         d_group(2)
-        out0_store(0, 1, "SSSS")
+        out0_store(0, 2, "SSSS")
         d_quantize(1)
         d_quantize(2)
 
         late_w = [(k, b) for k in range(TAPS) for b in (2, 3)]
-        for u in range(TAPS * PANELS):
+        for u in range(UNITS):
             b, k = divmod(u, TAPS)
-            if 2 <= u < 2 + len(late_w):
-                w_transpose(*late_w[u - 2])
-                w_copy(*late_w[u - 2])
-            if u >= TAPS * PANELS - 2:
-                jp = u - (TAPS * PANELS - 2)
-                out0_matmuls(1, jp)
-                out0_store(1, jp, "SVSV")
+            late = u - FIRST_LATE_UNIT
+            if 0 <= late < len(late_w):
+                w_transpose(*late_w[late])
+                w_copy(*late_w[late])
+            if u >= UNITS - 2:
+                j0 = 2 * (u - (UNITS - 2))
+                out0_matmuls(1, j0)
+                out0_store(1, j0, "SVSV")
             out1_unit(k, b, {0: "SSVS", 1: "SVSS"}.get(u, "SVSV"))
             if k == 0 and b + 1 < PANELS:
                 x_group(b + 1)
-            if 2 <= u < 2 + len(late_w) and u % 2 == 1:
-                w_quantize(*late_w[u - 3])
-                w_quantize(*late_w[u - 2])
+            if 0 <= late < len(late_w) and late % 2 == 1:
+                w_quantize(*late_w[late - 1])
+                w_quantize(*late_w[late])
             if k == 1 and b + 1 < PANELS:
                 x_quantize(b + 1)

from contextlib import ExitStack

import concourse.mybir as mybir
from concourse.masks import make_identity

TOKENS, E, C, TAPS = 512, 2048, 512, 3
FLOPS = 2 * 2 * TAPS * TOKENS * E * C

F32 = mybir.dt.float32
BF16 = mybir.dt.bfloat16
U32 = mybir.dt.uint32
U8 = mybir.dt.uint8
E4M3 = mybir.dt.float8_e4m3fn_x4
E5M2 = mybir.dt.float8_e5m2_x4
ACT = mybir.ActivationFunctionType
ALU = mybir.AluOpType

P = 128
PACK = 4
PANEL = 512
PANELS = E // PANEL
SLOTS = PACK + TAPS - 1
UNITS = TAPS * PANELS
FIRST_LATE_UNIT = 2


def tile_predictor_pa_v_kernel(tc, x, W1, b1, z, grad_out, out_0, out_1):
    nc = tc.nc
    with ExitStack() as ctx:
        ctx.enter_context(tc.manual_schedule())
        const = ctx.enter_context(tc.tile_pool(name="const", bufs=1))
        head = ctx.enter_context(tc.tile_pool(name="head", bufs=1))
        keep = ctx.enter_context(tc.tile_pool(name="keep", bufs=1))
        grouped = ctx.enter_context(tc.tile_pool(name="grouped", bufs=5))
        staged = ctx.enter_context(tc.tile_pool(name="staged", bufs=6))
        turned = ctx.enter_context(tc.psum_pool(name="turned", bufs=4))
        product = ctx.enter_context(tc.psum_pool(name="product", bufs=4))

        copy_on = {"S": nc.scalar.copy, "V": nc.vector.tensor_copy}

        g_sb = head.tile([P, PACK, C], BF16, name="g_sb")
        nc.sync.dma_start(out=g_sb[:], in_=grad_out.rearrange("(p j) c -> p j c", j=PACK))
        z_view = z.rearrange("(p j) c -> p j c", j=PACK)
        z_sb = []
        for i in range(2):
            z_half = head.tile([P, 2, C], F32, name="z%d" % i)
            nc.sync.dma_start(out=z_half[:], in_=z_view[:, 2 * i : 2 * i + 2, :])
            z_sb.append(z_half)

        w_sb = {}

        def load_w(k, h):
            pair = keep.tile([P, 2, PACK, C], BF16, name="w%d%d" % (k, h))
            rows = W1[k, 2 * PANEL * h : 2 * PANEL * (h + 1), :]
            nc.sync.dma_start(out=pair[:], in_=rows.rearrange("(b m r) c -> m b r c", b=2, r=PACK))
            for i in range(2):
                w_sb[(k, 2 * h + i)] = pair[:, i, :, :]

        for k in range(TAPS):
            load_w(k, 0)
        x_sb = keep.tile([P, PACK, E], BF16, name="x_sb")
        nc.sync.dma_start(out=x_sb[:], in_=x.rearrange("(p j) e -> p j e", j=PACK))
        for k in range(TAPS):
            load_w(k, 1)

        table_warmer = const.tile([P, 8], F32, name="table_warmer")
        nc.vector.memset(table_warmer[:], 0.0)
        nc.scalar.activation(out=table_warmer[:], in_=table_warmer[:], func=ACT.Tanh)
        ident = const.tile([P, P], F32, name="ident")
        make_identity(nc, ident[:])
        shift = const.tile([P, P], BF16, name="shift")
        nc.vector.memset(shift[:], 0.0)
        nc.vector.tensor_copy(out=shift[:, 0 : P - 1], in_=ident[:, 1:P])

        dz = keep.tile([P, SLOTS, C], BF16, name="dz")
        neg_g = head.tile([P, PACK, C], BF16, name="neg_g")
        nc.gpsimd.tensor_scalar(out=neg_g[:], in0=g_sb[:], scalar1=-1.0, scalar2=0.0, op0=ALU.mult, op1=ALU.add)
        tanh_sq = []
        for i in range(2):
            tanh_half = head.tile([P, 2, C], F32, name="tanh%d" % i)
            nc.scalar.activation(out=tanh_half[:], in_=z_sb[i][:], func=ACT.Tanh)
            tanh_sq.append(tanh_half)
        nc.vector.tensor_tensor(out=tanh_sq[0][:], in0=tanh_sq[0][:], in1=tanh_sq[0][:], op=ALU.mult)
        nc.scalar.activation(out=tanh_sq[1][:], in_=tanh_sq[1][:], func=ACT.Square)
        for i in range(2):
            nc.vector.scalar_tensor_tensor(
                out=dz[:, 2 * i : 2 * i + 2, :],
                in0=tanh_sq[i][:],
                scalar=1.0,
                in1=neg_g[:, 2 * i : 2 * i + 2, :],
                op0=ALU.subtract,
                op1=ALU.mult,
            )

        x_codes = keep.tile([P, E], U32, name="x_codes", align_bytes=64)
        x_scales = keep.tile([P, E], U8, name="x_scales", align_bytes=64)
        w_codes = []
        w_scales = []
        d_codes = []
        d_scales = []
        for k in range(TAPS):
            w_codes_k = keep.tile([P, E], U32, name="w_codes%d" % k, align_bytes=64)
            w_scales_k = keep.tile([P, E], U8, name="w_scales%d" % k, align_bytes=64)
            d_codes_k = keep.tile([P, C], U32, name="d_codes%d" % k, align_bytes=64)
            d_scales_k = keep.tile([P, C], U8, name="d_scales%d" % k, align_bytes=64)
            w_codes.append(w_codes_k)
            w_scales.append(w_scales_k)
            d_codes.append(d_codes_k)
            d_scales.append(d_scales_k)
        t_codes = keep.tile([P, SLOTS * P], U32, name="t_codes", align_bytes=64)
        t_scales = keep.tile([P, SLOTS * P], U8, name="t_scales", align_bytes=64)
        t_grouped = keep.tile([P, SLOTS * P * PACK], BF16, name="t_grouped", align_bytes=64)
        t_words = t_grouped[:].bitcast(F32).rearrange("p (s n v) -> p s n v", s=SLOTS, v=2)
        nc.vector.memset(t_grouped[:].rearrange("p (s n t) -> p s n t", s=SLOTS, t=PACK)[:, PACK:SLOTS, P - 1, :], 0.0)

        banks = {}
        laid_out = {}

        def shift_tokens():
            moved = turned.tile([P, 2 * C], BF16, name="moved", tag="bank")
            for j in range(2):
                nc.tensor.matmul(out=moved[:, C * j : C * (j + 1)], lhsT=shift[:], rhs=dz[:, j, :], start=True, stop=True)
            nc.scalar.copy(out=dz[:, PACK:SLOTS, :], in_=moved[:].rearrange("p (j c) -> p j c", j=2))

        def transpose_rows(bank, i, rows):
            words = rows.bitcast(F32)
            for v in range(2):
                nc.tensor.transpose(bank[:, P * (2 * i + v) : P * (2 * i + v + 1)], words[:, v : C // 2 : 2], ident[:])

        def dz_transpose(s0):
            bank = turned.tile([P, PACK * P], F32, name="dz_t", tag="bank")
            for i in range(2):
                transpose_rows(bank, i, dz[:, s0 + i, :])
            banks[("dz", s0)] = bank

        def dz_copy(s0):
            src = banks[("dz", s0 % PACK)][:].rearrange("p (s v n) -> p s n v", s=2, v=2)
            if s0 < PACK:
                nc.vector.tensor_copy(out=t_words[:, s0 : s0 + 2, :, :], in_=src)
            else:
                nc.vector.tensor_copy(out=t_words[:, s0 : s0 + 2, 0 : P - 1, :], in_=src[:, :, 1:P, :])

        def dz_quantize_features():
            own = PACK * P
            nc.vector.quantize_mx(
                out=t_codes[:, 0:own].bitcast(E5M2), scales=t_scales[:, 0:own], in_=t_grouped[:, 0 : PACK * own]
            )
            nc.vector.quantize_mx(
                out=t_codes[:, own:].bitcast(E5M2), scales=t_scales[:, own:], in_=t_grouped[:, PACK * own :]
            )

        def d_group(k):
            laid = grouped.tile([P, PACK * C], BF16, name="d_grouped", tag="grouped", align_bytes=64)
            nc.vector.tensor_copy(
                out=laid[:].rearrange("p (c t) -> p c t", t=PACK), in_=dz[:, k : k + PACK, :].rearrange("p t c -> p c t")
            )
            laid_out[("d", k)] = laid

        def d_quantize(k):
            nc.vector.quantize_mx(out=d_codes[k][:].bitcast(E5M2), scales=d_scales[k][:], in_=laid_out[("d", k)][:])

        def x_group(b):
            laid = grouped.tile([P, PACK * PANEL], BF16, name="x_grouped", tag="grouped", align_bytes=64)
            nc.vector.tensor_copy(
                out=laid[:].rearrange("p (r m t) -> p r m t", r=PACK, t=PACK),
                in_=x_sb[:, :, PANEL * b : PANEL * (b + 1)].rearrange("p t (m r) -> p r m t", r=PACK),
            )
            laid_out[("x", b)] = laid

        def x_quantize(b):
            cols = slice(PANEL * b, PANEL * (b + 1))
            nc.vector.quantize_mx(out=x_codes[:, cols].bitcast(E4M3), scales=x_scales[:, cols], in_=laid_out[("x", b)][:])

        def w_transpose(k, b):
            pair = []
            for half in range(2):
                bank = turned.tile([P, PACK * P], F32, name="w_t", tag="bank")
                for i in range(2):
                    transpose_rows(bank, i, w_sb[(k, b)][:, 2 * half + i, :])
                pair.append(bank)
            banks[("w", k, b)] = pair

        def w_copy(k, b):
            laid = grouped.tile([P, PACK * PANEL], BF16, name="w_grouped", tag="grouped", align_bytes=64)
            words = laid[:].bitcast(F32).rearrange("p (m r v) -> p m r v", r=PACK, v=2)
            for half in range(2):
                nc.scalar.copy(
                    out=words[:, :, 2 * half : 2 * half + 2, :],
                    in_=banks[("w", k, b)][half][:].rearrange("p (r v m) -> p m r v", r=2, v=2),
                )
            laid_out[("w", k, b)] = laid

        def w_quantize(k, b):
            cols = slice(PANEL * b, PANEL * (b + 1))
            nc.vector.quantize_mx(
                out=w_codes[k][:, cols].bitcast(E4M3), scales=w_scales[k][:, cols], in_=laid_out[("w", k, b)][:]
            )

        def out1_unit(k, b, engines):
            four = []
            for r in range(PACK):
                bank = product.tile([P, C], F32, name="bank", tag="bank")
                cols = slice(PANEL * b + P * r, PANEL * b + P * (r + 1))
                nc.tensor.matmul_mx(
                    out=bank[:],
                    lhsT=x_codes[:, cols].bitcast(E4M3),
                    lhsT_scale=x_scales[:, cols],
                    rhs=d_codes[k][:].bitcast(E5M2),
                    rhs_scale=d_scales[k][:],
                    start=True,
                    stop=True,
                )
                four.append(bank)
            st = staged.tile([P, PACK, C], F32, name="st", tag="st")
            for r in range(PACK):
                copy_on[engines[r]](out=st[:, r, :], in_=four[r][:])
            nc.sync.dma_start(
                out=out_1[k, PANEL * b : PANEL * (b + 1), :].rearrange("(m r) c -> m r c", r=PACK), in_=st[:]
            )

        out_0_view = out_0.rearrange("(n j) e -> n j e", j=PACK)

        def out0_matmuls(h, j0):
            four = []
            for j in (j0, j0 + 1):
                for b in (2 * h, 2 * h + 1):
                    bank = product.tile([P, PANEL], F32, name="bank", tag="bank")
                    e_cols = slice(PANEL * b, PANEL * (b + 1))
                    for k in range(TAPS):
                        t_cols = slice(P * (j + k), P * (j + k + 1))
                        nc.tensor.matmul_mx(
                            out=bank[:],
                            lhsT=t_codes[:, t_cols].bitcast(E5M2),
                            lhsT_scale=t_scales[:, t_cols],
                            rhs=w_codes[k][:, e_cols].bitcast(E4M3),
                            rhs_scale=w_scales[k][:, e_cols],
                            start=(k == 0),
                            stop=(k == TAPS - 1),
                        )
                    four.append(bank)
            banks[("out0", h, j0)] = four

        def out0_store(h, j0, engines):
            st = staged.tile([P, 2, 2 * PANEL], F32, name="st", tag="st")
            for i in range(2):
                for side in range(2):
                    copy_on[engines[2 * i + side]](
                        out=st[:, i, PANEL * side : PANEL * (side + 1)], in_=banks[("out0", h, j0)][2 * i + side][:]
                    )
                nc.sync.dma_start(out=out_0_view[:, j0 + i, 2 * PANEL * h : 2 * PANEL * (h + 1)], in_=st[:, i, :])

        for k in range(TAPS):
            for b in range(2):
                w_transpose(k, b)
                w_copy(k, b)
            if k == 0:
                shift_tokens()
                dz_transpose(0)
                dz_transpose(2)
                d_group(0)
                dz_copy(0)
                dz_copy(PACK)
                dz_copy(2)
            else:
                w_quantize(k - 1, 0)
                w_quantize(k - 1, 1)
            if k == 1:
                dz_quantize_features()
        w_quantize(TAPS - 1, 0)
        w_quantize(TAPS - 1, 1)

        out0_matmuls(0, 0)
        d_quantize(0)
        out0_store(0, 0, "SSSS")
        x_group(0)
        d_group(1)
        x_quantize(0)
        out0_matmuls(0, 2)
        d_group(2)
        out0_store(0, 2, "SSSS")
        d_quantize(1)
        d_quantize(2)

        late_w = [(k, b) for k in range(TAPS) for b in (2, 3)]
        for u in range(UNITS):
            b, k = divmod(u, TAPS)
            late = u - FIRST_LATE_UNIT
            if 0 <= late < len(late_w):
                w_transpose(*late_w[late])
                w_copy(*late_w[late])
            if u >= UNITS - 2:
                j0 = 2 * (u - (UNITS - 2))
                out0_matmuls(1, j0)
                out0_store(1, j0, "SVSV")
            out1_unit(k, b, {0: "SSVS", 1: "SVSS"}.get(u, "SVSV"))
            if k == 0 and b + 1 < PANELS:
                x_group(b + 1)
            if 0 <= late < len(late_w) and late % 2 == 1:
                w_quantize(*late_w[late - 1])
                w_quantize(*late_w[late])
            if k == 1 and b + 1 < PANELS:
                x_quantize(b + 1)
